import numpy as np
import ml_dtypes


def mxq(x, axis, fmt="e4m3"):
    dtype, down = {"e4m3": (ml_dtypes.float8_e4m3fn, 7), "e5m2": (ml_dtypes.float8_e5m2, 14)}[fmt]
    v = np.moveaxis(np.asarray(x, np.float32).astype(ml_dtypes.bfloat16).astype(np.float64), axis, -1)
    blocks = v.reshape(v.shape[:-1] + (-1, 32))
    amax = np.abs(blocks).max(-1, keepdims=True)
    byte = np.maximum(np.where(amax > 0, np.frexp(amax)[1] - 1 + 127, 0) - down, 1)
    scale = np.exp2(byte - 127.0)
    codes = (blocks / scale).astype(np.float32).astype(dtype).astype(np.float64)
    return np.moveaxis((codes * scale).reshape(v.shape), -1, axis)


WIDE = False


def mx_kscale(k):
    if not WIDE:
        return np.ones(k)
    levels = np.array([10, -10, 5, -5, 0])
    if k % 512:
        return np.exp2(np.random.permutation(np.resize(levels, k // 32))).repeat(32)
    a = np.empty((k // 512, 16))
    for p in range(k // 512):
        a[p, :8] = np.random.permutation(np.resize(levels, 8))
        for g in range(8):
            far = levels[np.abs(levels - a[p, g]) >= 10]
            a[p, g + 8] = far[np.random.randint(len(far))]
    return np.exp2(a.ravel()).repeat(32)


BF16 = ml_dtypes.bfloat16


def bf(x):
    return np.asarray(x, np.float32).astype(BF16)


def f64(x):
    return np.asarray(x).astype(np.float64)


B, T, H, D = 32, 128, 2, 1024
A = 1.5 / D ** 0.25


def relative_shift(x):
    b, h, t, tt = x.shape
    x = np.pad(x, [[0, 0], [0, 0], [0, 0], [1, 0]])
    x = x.reshape(b, h, tt + 1, t)[:, :, 1:, :]
    return x.reshape(b, h, t, tt)


def setup_inputs():
    s = mx_kscale(D)
    return {"q": bf(np.random.standard_normal((B, T, H, D)) * A * s),
            "k": bf(np.random.standard_normal((B, T, H, D)) * A / s),
            "r_w_bias": bf(np.random.standard_normal((H, D)) * 0.5 * A * s),
            "r_r_bias": bf(np.random.standard_normal((H, D)) * 0.5 * A * s),
            "rel_pos_emb": bf(np.random.standard_normal((T, H, D)) * A / s)}


def reference(q, k, r_w_bias, r_r_bias, rel_pos_emb):
    qw = (f64(q) + f64(r_w_bias)).transpose(0, 2, 1, 3)
    qr = (f64(q) + f64(r_r_bias)).transpose(0, 2, 1, 3)
    kt = f64(k).transpose(0, 2, 3, 1)
    rt = f64(rel_pos_emb).transpose(1, 2, 0)
    content = mxq(qw, 3, "e4m3") @ mxq(kt, 2, "e4m3")
    rel = mxq(qr, 3, "e4m3") @ mxq(rt, 1, "e4m3")
    return content + relative_shift(rel)

@@ -1,0 +1,376 @@
+from contextlib import ExitStack
+
+import concourse.mybir as mybir
+from concourse.masks import make_identity
+
+F32 = mybir.dt.float32
+BF16 = mybir.dt.bfloat16
+U32 = mybir.dt.uint32
+U8 = mybir.dt.uint8
+FP8X4 = mybir.dt.float8_e4m3fn_x4
+ADD = mybir.AluOpType.add
+IDENTITY = mybir.ActivationFunctionType.Identity
+
+B, T, H, D = 32, 128, 2, 1024
+P = 128
+FLOPS = 2 * 2 * B * H * T * T * D
+
+GROUP = 4
+NGROUPS = B * H // GROUP
+SLOT = (T + 1) * T
+NSTG = 3
+
+NF = B - 4
+TAIL = 4
+PF = 3
+PERIOD = 3
+FIRST_SPECIAL = PERIOD + PF
+
+
+def is_special(b):
+    return FIRST_SPECIAL <= b < NF and b % PERIOD == FIRST_SPECIAL % PERIOD
+
+
+def c_step(b):
+    return b if b < NF else b + TAIL
+
+
+def fa_step(gi):
+    return {12: 30, 13: 34, 14: 35, 15: 37}.get(gi, 2 * gi + 5)
+
+
+def transpose_head(nc, bank, words, ident):
+    for u in range(2):
+        for g in range(2):
+            c = 2 * u + g
+            nc.tensor.transpose(
+                bank[:, 128 * c : 128 * c + 128], words[:, 256 * g + u : 256 * (g + 1) : 2], ident
+            )
+
+
+def leave_bank(nc, dst_words, bank):
+    nc.scalar.copy(
+        out=dst_words.rearrange("p (x u) -> p x u", u=2),
+        in_=bank[:].rearrange("p (u x) -> p x u", u=2),
+    )
+
+
+def tile_relativepositionembedding_pa_t_kernel(tc, q, k, r_w_bias, r_r_bias, rel_pos_emb, out):
+    nc = tc.nc
+    out_flat = out.rearrange("b h t j -> (b h t j)")
+    with ExitStack() as ctx:
+        const = ctx.enter_context(tc.tile_pool(name="const", bufs=1))
+        io = ctx.enter_context(tc.tile_pool(name="io", bufs=PF + 2))
+        rawp = ctx.enter_context(tc.tile_pool(name="rawp", bufs=TAIL + 1))
+        work = ctx.enter_context(tc.tile_pool(name="work", bufs=3))
+        codes = ctx.enter_context(tc.tile_pool(name="codes", bufs=7))
+        back_pool = ctx.enter_context(tc.tile_pool(name="backp", bufs=3))
+        psum = ctx.enter_context(tc.psum_pool(name="psum", bufs=2))
+        ctx.enter_context(tc.manual_schedule())
+
+        ident = const.tile([P, P], F32)
+        make_identity(nc, ident[:])
+
+        brow = const.tile([P, D], BF16)
+        nc.vector.memset(brow[:], 0.0)
+        nc.sync.dma_start(out=brow[0:2, :], in_=r_w_bias)
+        nc.sync.dma_start(out=brow[2:4, :], in_=r_r_bias)
+
+        qts = {}
+        qss = {}
+        kts = {}
+
+        def load_q(b):
+            if 0 <= b < B:
+                qt = io.tile([P, H * D], BF16, tag="q")
+                if is_special(b):
+                    nc.sync.dma_start(out=qt[:, 0:D], in_=q[b][:, 0, :])
+                else:
+                    nc.sync.dma_start(out=qt[:], in_=q[b].rearrange("t h d -> t (h d)"))
+                qts[b] = qt
+
+        def load_q_special(b):
+            if is_special(b):
+                qh = io.tile([P, D], BF16, tag="qh", bufs=2)
+                nc.sync.dma_start(out=qh[:], in_=q[b][:, 1, :])
+                qss[b] = qh
+
+        def load_k(b):
+            if 0 <= b < B:
+                kt = io.tile([P, H * D], BF16, tag="k")
+                nc.sync.dma_start(out=kt[:], in_=k[b].rearrange("t h d -> t (h d)"))
+                kts[b] = kt
+
+        load_q(0)
+        load_k(0)
+        rsb = const.tile([P, H * D], BF16)
+        nc.sync.dma_start(out=rsb[:], in_=rel_pos_emb.rearrange("j h d -> j (h d)"))
+        for b in range(1, PF):
+            load_q(b)
+            load_k(b)
+
+        stg = []
+        for s in range(NSTG):
+            st = const.tile([P, GROUP * (T + 1)], F32, name="stg%d" % s)
+            nc.vector.memset(st[:], 0.0)
+            stg.append(st)
+
+        pb = psum.tile([P, 512], F32, tag="xk")
+        brow_w = brow[:].bitcast(F32)
+        for c in range(4):
+            first = 256 * (c // 2) + c % 2
+            nc.tensor.transpose(
+                pb[:, 128 * c : 128 * c + 128], brow_w[:, first : 256 * (c // 2 + 1) : 2], ident[:]
+            )
+        bsm = const.tile([P, 16], F32)
+        nc.vector.tensor_copy(
+            out=bsm[:].rearrange("p (i c) -> p i c", c=4),
+            in_=pb[:].rearrange("p (c i) -> p i c", c=4)[:, 0:4, :],
+        )
+        bfull = const.tile([P, 4 * D], BF16, align_bytes=64)
+        bfull_w = bfull[:].bitcast(F32)
+        for i in (2, 0, 3, 1):
+            nc.vector.tensor_copy(
+                out=bfull_w[:, 512 * i : 512 * i + 512].rearrange("p (g r u) -> p g r u", g=2, u=2),
+                in_=bsm[:, 4 * i : 4 * i + 4].rearrange("p (g u) -> p g u", g=2).unsqueeze(2).to_broadcast([P, 2, T, 2]),
+            )
+        b32 = const.tile([P, 32], F32)
+        nc.vector.tensor_copy(out=b32[:], in_=bsm[:].bitcast(BF16))
+
+        gr = const.tile([P, H * D], BF16, align_bytes=64)
+        rc = const.tile([P, 512], U32, align_bytes=64)
+        rs = const.tile([P, 512], U8, align_bytes=64)
+
+        def prepare_r_tensor():
+            gr_w = gr[:].bitcast(F32)
+            rsb_w = rsb[:].bitcast(F32)
+            for h in range(H):
+                xr = psum.tile([P, 512], F32, tag="xk")
+                transpose_head(nc, xr, rsb_w[:, 512 * h : 512 * h + 512], ident[:])
+                leave_bank(nc, gr_w[:, 512 * h : 512 * h + 512], xr)
+
+        xqs = {}
+        xss = {}
+        raws = {}
+        gks = {}
+        gts = {}
+        cod = {("e", 0): (rc, rs, 0)}
+        rels = {}
+        conts = {}
+        rbs = {}
+        fins = {}
+
+        def turn_q(b):
+            if not 0 <= b < B:
+                return
+            words = qts[b][:].bitcast(F32)
+            if b >= NF:
+                raw = rawp.tile([P, H * 512], F32, tag="raw")
+                raws[b] = raw
+            for h in range(H):
+                if h == 1 and is_special(b):
+                    continue
+                xq = psum.tile([P, 512], F32, tag="xq")
+                transpose_head(nc, xq, words[:, 512 * h : 512 * h + 512], ident[:])
+                if b >= NF:
+                    leave_bank(nc, raws[b][:, 512 * h : 512 * h + 512], xq)
+                else:
+                    xqs[(b, h)] = xq
+
+        def turn_special(b):
+            if is_special(b):
+                xs = psum.tile([P, 512], F32, tag="xs")
+                transpose_head(nc, xs, qss[b][:].bitcast(F32), ident[:])
+                xss[b] = xs
+                gs = work.tile([P, 4 * D], BF16, tag="gs", bufs=2, align_bytes=64)
+                gts[b] = gs
+
+        def turn_k(b):
+            words = kts[b][:].bitcast(F32)
+            gk = work.tile([P, H * D], BF16, tag="gk", align_bytes=64)
+            gk_w = gk[:].bitcast(F32)
+            for h in range(H):
+                xk = psum.tile([P, 512], F32, tag="xk")
+                transpose_head(nc, xk, words[:, 512 * h : 512 * h + 512], ident[:])
+                leave_bank(nc, gk_w[:, 512 * h : 512 * h + 512], xk)
+            gks[b] = gk
+
+        def sums(s):
+            if 0 <= s < NF:
+                if not is_special(s):
+                    g_new = work.tile([P, 4 * D], BF16, tag="g", align_bytes=64)
+                    gts[s] = g_new
+                for h in range(H):
+                    if h == 1 and is_special(s):
+                        continue
+                    bank = xqs[(s, h)][:].bitcast(BF16).rearrange("p (u x e) -> p x u e", u=2, e=2)
+                    for side in range(2):
+                        i = 2 * (1 - side) + h
+                        o = D * (2 * side + h)
+                        nc.vector.tensor_tensor(
+                            out=gts[s][:, o : o + D].rearrange("p (x u e) -> p x u e", u=2, e=2),
+                            in0=bank,
+                            in1=bfull[:, D * i : D * i + D].rearrange("p (x u e) -> p x u e", u=2, e=2),
+                            op=ADD,
+                        )
+            for side, b in ((0, s), (1, s - TAIL)):
+                if NF <= b < B:
+                    g_tail = work.tile([P, 4 * D], BF16, tag="g", align_bytes=64)
+                    i = 2 * (1 - side)
+                    nc.vector.tensor_tensor(
+                        out=g_tail[:, 0 : H * D], in0=raws[b][:].bitcast(BF16), in1=bfull[:, D * i : D * i + H * D], op=ADD
+                    )
+                    gts[(side, b)] = g_tail
+
+        def quantise_q(src, width):
+            cq = codes.tile([P, D], U32, tag="cq", align_bytes=64)
+            sq = codes.tile([P, D], U8, tag="sq", align_bytes=64)
+            nc.vector.quantize_mx(
+                out=cq[:, 0 : width // 4].bitcast(FP8X4), scales=sq[:, 0 : width // 4], in_=src[:, 0:width]
+            )
+            return cq, sq
+
+        def quantise_k(b):
+            ck = codes.tile([P, 512], U32, tag="ck", align_bytes=64)
+            sk = codes.tile([P, 512], U8, tag="sk", align_bytes=64)
+            nc.vector.quantize_mx(out=ck[:].bitcast(FP8X4), scales=sk[:], in_=gks[b][:])
+            cod[("k", b)] = (ck, sk, 0)
+
+        def quants(j):
+            if 0 <= j < NF:
+                cq, sq = quantise_q(gts[j], 4 * D)
+                cod[("r", j)] = (cq, sq, 0)
+                cod[("w", j)] = (cq, sq, 512)
+                quantise_k(j)
+            if NF <= j < B:
+                cq, sq = quantise_q(gts[(0, j)], H * D)
+                cod[("r", j)] = (cq, sq, 0)
+            if NF <= j - TAIL < B:
+                cq, sq = quantise_q(gts[(1, j - TAIL)], H * D)
+                cod[("w", j - TAIL)] = (cq, sq, 0)
+                quantise_k(j - TAIL)
+
+        def multiply(bank, b, left, right):
+            lc, ls, lb = left
+            mc, ms, mb = right
+            for h in range(H):
+                i = 2 * (b % 2) + h
+                for g in range(2):
+                    a = lb + 128 * (2 * h + g)
+                    m = mb + 128 * (2 * h + g)
+                    nc.tensor.matmul_mx(
+                        out=bank[:, 128 * i : 128 * i + 128],
+                        lhsT=lc[:, a : a + 128].bitcast(FP8X4),
+                        lhsT_scale=ls[:, a : a + 128],
+                        rhs=mc[:, m : m + 128].bitcast(FP8X4),
+                        rhs_scale=ms[:, m : m + 128],
+                        start=(g == 0),
+                        stop=(g == 1),
+                    )
+
+        def mult_rel(b):
+            if 0 <= b < B:
+                if b % 2 == 0:
+                    rel_new = psum.tile([P, 512], F32, tag="rel", bufs=1)
+                    rels[b // 2] = rel_new
+                multiply(rels[b // 2], b, cod[("r", b)], cod[("e", 0)])
+
+        def mult_content(gi):
+            cont = psum.tile([P, 512], F32, tag="cont", bufs=1)
+            for b in (2 * gi, 2 * gi + 1):
+                multiply(cont, b, cod[("w", b)], cod[("k", b)])
+            conts[gi] = cont
+
+        def offload(s):
+            for b in range(s + 1, s + PERIOD + 1):
+                if is_special(b):
+                    part = s - (b - PERIOD)
+                    bank = xss[b][:].bitcast(BF16).rearrange("p (c r e) -> p c r e", c=4, e=2)
+                    for idx in range(16 * part // PERIOD, 16 * (part + 1) // PERIOD):
+                        side = idx // 8
+                        g = (idx // 4) % 2
+                        u = (idx // 2) % 2
+                        e = idx % 2
+                        col = 8 * (2 * (1 - side) + 1) + 4 * g + 2 * u + e
+                        o = D * (2 * side + 1) + 512 * g
+                        nc.scalar.activation(
+                            out=gts[b][:, o : o + 512].rearrange("p (r j) -> p r j", j=4)[:, :, 2 * u + e],
+                            in_=bank[:, 2 * u + g, :, e],
+                            func=IDENTITY,
+                            bias=b32[:, col : col + 1],
+                            scale=1.0,
+                        )
+
+        def area_of(gi):
+            base = min(GROUP * SLOT * gi, B * H * T * T - GROUP * SLOT)
+            return out_flat[base : base + GROUP * SLOT]
+
+        def pad_rel(gi):
+            nc.scalar.copy(
+                out=stg[gi % NSTG][:].rearrange("p (i c) -> p i c", i=GROUP)[:, :, 1 : T + 1],
+                in_=rels[gi][:].rearrange("p (i j) -> p i j", i=GROUP),
+            )
+
+        def park(gi):
+            nc.sync.dma_start(
+                out=area_of(gi).rearrange("(i t c) -> t i c", i=GROUP, t=T),
+                in_=stg[gi % NSTG][:].rearrange("p (i c) -> p i c", i=GROUP),
+            )
+
+        def fetch(gi):
+            rb = back_pool.tile([P, GROUP * T], F32, tag="rb")
+            nc.sync.dma_start(
+                out=rb[:].rearrange("p (i j) -> p i j", i=GROUP),
+                in_=area_of(gi).rearrange("(i f) -> i f", i=GROUP)[:, T:SLOT].rearrange("i (t j) -> t i j", t=T),
+            )
+            rbs[gi] = rb
+
+        def final_add(gi):
+            fin = back_pool.tile([P, GROUP * T], F32, tag="fin")
+            nc.vector.tensor_tensor(out=fin[:], in0=conts[gi][:], in1=rbs[gi][:], op=ADD)
+            fins[gi] = fin
+
+        def final_store(gi):
+            nc.sync.dma_start(
+                out=out[2 * gi : 2 * gi + 2].rearrange("b h t j -> t (b h) j"),
+                in_=fins[gi][:].rearrange("p (i j) -> p i j", i=GROUP),
+            )
+
+        groups = range(NGROUPS)
+        for s in range(-1, fa_step(NGROUPS - 1) + 1):
+            load_q(s + 1 + PF)
+            for b in range(PF, B):
+                if c_step(b) == s + 1 + PF:
+                    load_k(b)
+            load_q_special(s + PERIOD + PF)
+            due = [gi for gi in groups if fa_step(gi) == s]
+            padded = [gi for gi in groups if 2 * gi + 3 == s]
+            for gi in due:
+                mult_content(gi)
+            for gi in padded:
+                pad_rel(gi)
+            next_k = [b for b in range(B) if c_step(b) == s + 1]
+            if s >= 0:
+                for b in next_k:
+                    turn_k(b)
+            turn_special(s + PERIOD)
+            sums(s)
+            turn_q(s + 1)
+            if s == -1:
+                for b in next_k:
+                    turn_k(b)
+                prepare_r_tensor()
+            if s == 1:
+                nc.vector.quantize_mx(out=rc[:].bitcast(FP8X4), scales=rs[:], in_=gr[:])
+            quants(s - 1)
+            mult_rel(s - 1)
+            offload(s)
+            for gi in due:
+                final_add(gi)
+            for gi in groups:
+                if 2 * gi + 4 == s:
+                    fetch(gi)
+            for gi in padded:
+                park(gi)
+            for gi in due:
+                final_store(gi)

@@ -39,6 +39,10 @@ def fa_step(gi):
     return {12: 30, 13: 34, 14: 35, 15: 37}.get(gi, 2 * gi + 5)
 
 
+def on_gpsimd(gi):
+    return gi < NGROUPS - 2
+
+
 def transpose_head(nc, bank, words, ident):
     for u in range(2):
         for g in range(2):
@@ -158,6 +162,7 @@ def tile_relativepositionembedding_pa_t_kernel(tc, q, k, r_w_bias, r_r_bias, rel
         rels = {}
         conts = {}
         rbs = {}
+        css = {}
         fins = {}
 
         def turn_q(b):
@@ -325,9 +330,17 @@ def tile_relativepositionembedding_pa_t_kernel(tc, q, k, r_w_bias, r_r_bias, rel
             )
             rbs[gi] = rb
 
+        def move_content(gi):
+            cs = back_pool.tile([P, GROUP * T], F32, tag="cs")
+            nc.scalar.copy(out=cs[:], in_=conts[gi][:])
+            css[gi] = cs
+
         def final_add(gi):
             fin = back_pool.tile([P, GROUP * T], F32, tag="fin")
-            nc.vector.tensor_tensor(out=fin[:], in0=conts[gi][:], in1=rbs[gi][:], op=ADD)
+            if on_gpsimd(gi):
+                nc.gpsimd.tensor_tensor(out=fin[:], in0=css[gi][:], in1=rbs[gi][:], op=ADD)
+            else:
+                nc.vector.tensor_tensor(out=fin[:], in0=conts[gi][:], in1=rbs[gi][:], op=ADD)
             fins[gi] = fin
 
         def final_store(gi):
@@ -345,7 +358,8 @@ def tile_relativepositionembedding_pa_t_kernel(tc, q, k, r_w_bias, r_r_bias, rel
             load_q_special(s + PERIOD + PF)
             due = [gi for gi in groups if fa_step(gi) == s]
             padded = [gi for gi in groups if 2 * gi + 3 == s]
-            for gi in due:
+            early = [gi for gi in groups if on_gpsimd(gi) and 2 * gi + 4 == s]
+            for gi in early + [gi for gi in due if not on_gpsimd(gi)]:
                 mult_content(gi)
             for gi in padded:
                 pad_rel(gi)
@@ -353,6 +367,8 @@ def tile_relativepositionembedding_pa_t_kernel(tc, q, k, r_w_bias, r_r_bias, rel
             if s >= 0:
                 for b in next_k:
                     turn_k(b)
+            for gi in early:
+                move_content(gi)
             turn_special(s + PERIOD)
             sums(s)
             turn_q(s + 1)

@@ -16,34 +16,19 @@ P = 128
 FLOPS = 2 * 2 * B * H * T * T * D
 
 GROUP = 4
-NGROUPS = B * H // GROUP
+NG = B * H // GROUP
+NM = NG - 2
 SLOT = (T + 1) * T
 NSTG = 3
-
-NF = B - 4
-TAIL = 4
 PF = 3
-PERIOD = 3
-FIRST_SPECIAL = PERIOD + PF
+GW = 2 * H * D
 
 
-def is_special(b):
-    return FIRST_SPECIAL <= b < NF and b % PERIOD == FIRST_SPECIAL % PERIOD
+def words_of(q_words, pair):
+    return q_words[:, 512 * pair : 512 * pair + 512]
 
 
-def c_step(b):
-    return b if b < NF else b + TAIL
-
-
-def fa_step(gi):
-    return {12: 30, 13: 34, 14: 35, 15: 37}.get(gi, 2 * gi + 5)
-
-
-def on_gpsimd(gi):
-    return gi < NGROUPS - 2
-
-
-def transpose_head(nc, bank, words, ident):
+def transpose_pair(nc, bank, words, ident):
     for u in range(2):
         for g in range(2):
             c = 2 * u + g
@@ -64,10 +49,10 @@ def tile_relativepositionembedding_pa_t_kernel(tc, q, k, r_w_bias, r_r_bias, rel
     out_flat = out.rearrange("b h t j -> (b h t j)")
     with ExitStack() as ctx:
         const = ctx.enter_context(tc.tile_pool(name="const", bufs=1))
-        io = ctx.enter_context(tc.tile_pool(name="io", bufs=PF + 2))
-        rawp = ctx.enter_context(tc.tile_pool(name="rawp", bufs=TAIL + 1))
-        work = ctx.enter_context(tc.tile_pool(name="work", bufs=3))
-        codes = ctx.enter_context(tc.tile_pool(name="codes", bufs=7))
+        io = ctx.enter_context(tc.tile_pool(name="io", bufs=PF + 1))
+        rawp = ctx.enter_context(tc.tile_pool(name="rawp", bufs=2))
+        work = ctx.enter_context(tc.tile_pool(name="work", bufs=2))
+        codes = ctx.enter_context(tc.tile_pool(name="codes", bufs=3))
         back_pool = ctx.enter_context(tc.tile_pool(name="backp", bufs=3))
         psum = ctx.enter_context(tc.psum_pool(name="psum", bufs=2))
         ctx.enter_context(tc.manual_schedule())
@@ -75,48 +60,49 @@ def tile_relativepositionembedding_pa_t_kernel(tc, q, k, r_w_bias, r_r_bias, rel
         ident = const.tile([P, P], F32)
         make_identity(nc, ident[:])
 
-        brow = const.tile([P, D], BF16)
-        nc.vector.memset(brow[:], 0.0)
-        nc.sync.dma_start(out=brow[0:2, :], in_=r_w_bias)
-        nc.sync.dma_start(out=brow[2:4, :], in_=r_r_bias)
-
         qts = {}
-        qss = {}
         kts = {}
 
-        def load_q(b):
-            if 0 <= b < B:
-                qt = io.tile([P, H * D], BF16, tag="q")
-                if is_special(b):
-                    nc.sync.dma_start(out=qt[:, 0:D], in_=q[b][:, 0, :])
-                else:
-                    nc.sync.dma_start(out=qt[:], in_=q[b].rearrange("t h d -> t (h d)"))
-                qts[b] = qt
+        def load_q(m, pieces=1):
+            if m < NG:
+                qt = io.tile([P, GW], BF16, tag="q")
+                qts[m] = qt
+                if pieces == 1:
+                    nc.sync.dma_start(
+                        out=qt[:].rearrange("p (b x) -> p b x", b=2),
+                        in_=q[2 * m : 2 * m + 2].rearrange("b t h d -> t b (h d)"),
+                    )
 
-        def load_q_special(b):
-            if is_special(b):
-                qh = io.tile([P, D], BF16, tag="qh", bufs=2)
-                nc.sync.dma_start(out=qh[:], in_=q[b][:, 1, :])
-                qss[b] = qh
+        def load_k(m):
+            if m < NG:
+                kt = io.tile([P, GW], BF16, tag="k")
+                nc.sync.dma_start(
+                    out=kt[:].rearrange("p (b x) -> p b x", b=2),
+                    in_=k[2 * m : 2 * m + 2].rearrange("b t h d -> t b (h d)"),
+                )
+                kts[m] = kt
 
-        def load_k(b):
-            if 0 <= b < B:
-                kt = io.tile([P, H * D], BF16, tag="k")
-                nc.sync.dma_start(out=kt[:], in_=k[b].rearrange("t h d -> t (h d)"))
-                kts[b] = kt
+        brow = const.tile([P, D], BF16)
+        nc.vector.memset(brow[:].bitcast(F32), 0.0)
 
-        load_q(0)
+        load_q(0, pieces=2)
+        nc.sync.dma_start(out=qts[0][:, 0:D], in_=q[0][:, 0, :])
+        nc.sync.dma_start(out=brow[0:2, :], in_=r_r_bias)
+        nc.sync.dma_start(out=brow[2:4, :], in_=r_w_bias)
+        nc.sync.dma_start(out=qts[0][:, D : 2 * D], in_=q[0][:, 1, :])
+        nc.sync.dma_start(out=qts[0][:, 2 * D : 4 * D], in_=q[1].rearrange("t h d -> t (h d)"))
+        load_q(1)
         load_k(0)
         rsb = const.tile([P, H * D], BF16)
         nc.sync.dma_start(out=rsb[:], in_=rel_pos_emb.rearrange("j h d -> j (h d)"))
-        for b in range(1, PF):
-            load_q(b)
-            load_k(b)
+        load_k(1)
+        load_q(2)
+        load_k(2)
 
         stg = []
         for s in range(NSTG):
             st = const.tile([P, GROUP * (T + 1)], F32, name="stg%d" % s)
-            nc.vector.memset(st[:], 0.0)
+            nc.gpsimd.memset(st[:], 0.0)
             stg.append(st)
 
         pb = psum.tile([P, 512], F32, tag="xk")
@@ -133,11 +119,17 @@ def tile_relativepositionembedding_pa_t_kernel(tc, q, k, r_w_bias, r_r_bias, rel
         )
         bfull = const.tile([P, 4 * D], BF16, align_bytes=64)
         bfull_w = bfull[:].bitcast(F32)
-        for i in (2, 0, 3, 1):
-            nc.vector.tensor_copy(
+
+        def widen(copy, i):
+            copy(
                 out=bfull_w[:, 512 * i : 512 * i + 512].rearrange("p (g r u) -> p g r u", g=2, u=2),
                 in_=bsm[:, 4 * i : 4 * i + 4].rearrange("p (g u) -> p g u", g=2).unsqueeze(2).to_broadcast([P, 2, T, 2]),
             )
+
+        widen(nc.vector.tensor_copy, 0)
+        widen(nc.scalar.copy, 2)
+        widen(nc.vector.tensor_copy, 1)
+        widen(nc.scalar.copy, 3)
         b32 = const.tile([P, 32], F32)
         nc.vector.tensor_copy(out=b32[:], in_=bsm[:].bitcast(BF16))
 
@@ -145,248 +137,302 @@ def tile_relativepositionembedding_pa_t_kernel(tc, q, k, r_w_bias, r_r_bias, rel
         rc = const.tile([P, 512], U32, align_bytes=64)
         rs = const.tile([P, 512], U8, align_bytes=64)
 
-        def prepare_r_tensor():
-            gr_w = gr[:].bitcast(F32)
-            rsb_w = rsb[:].bitcast(F32)
+        def prepare_r():
             for h in range(H):
                 xr = psum.tile([P, 512], F32, tag="xk")
-                transpose_head(nc, xr, rsb_w[:, 512 * h : 512 * h + 512], ident[:])
-                leave_bank(nc, gr_w[:, 512 * h : 512 * h + 512], xr)
+                transpose_pair(nc, xr, words_of(rsb[:].bitcast(F32), h), ident[:])
+                leave_bank(nc, words_of(gr[:].bitcast(F32), h), xr)
 
-        xqs = {}
-        xss = {}
+        banks = {}
+        shared = {}
         raws = {}
-        gks = {}
+        small = {}
         gts = {}
-        cod = {("e", 0): (rc, rs, 0)}
+        gks = {}
+        cod = {}
         rels = {}
         conts = {}
-        rbs = {}
         css = {}
+        rbs = {}
         fins = {}
 
-        def turn_q(b):
-            if not 0 <= b < B:
-                return
-            words = qts[b][:].bitcast(F32)
-            if b >= NF:
-                raw = rawp.tile([P, H * 512], F32, tag="raw")
-                raws[b] = raw
-            for h in range(H):
-                if h == 1 and is_special(b):
-                    continue
+        def turn_q(m, pair):
+            if m < NM:
                 xq = psum.tile([P, 512], F32, tag="xq")
-                transpose_head(nc, xq, words[:, 512 * h : 512 * h + 512], ident[:])
-                if b >= NF:
-                    leave_bank(nc, raws[b][:, 512 * h : 512 * h + 512], xq)
-                else:
-                    xqs[(b, h)] = xq
+                transpose_pair(nc, xq, words_of(qts[m][:].bitcast(F32), pair), ident[:])
+                banks[(m, pair)] = xq
 
-        def turn_special(b):
-            if is_special(b):
+        def turn_shared(m):
+            if m < NM:
                 xs = psum.tile([P, 512], F32, tag="xs")
-                transpose_head(nc, xs, qss[b][:].bitcast(F32), ident[:])
-                xss[b] = xs
-                gs = work.tile([P, 4 * D], BF16, tag="gs", bufs=2, align_bytes=64)
-                gts[b] = gs
+                transpose_pair(nc, xs, words_of(qts[m][:].bitcast(F32), 3), ident[:])
+                shared[m] = xs
 
-        def turn_k(b):
-            words = kts[b][:].bitcast(F32)
-            gk = work.tile([P, H * D], BF16, tag="gk", align_bytes=64)
-            gk_w = gk[:].bitcast(F32)
-            for h in range(H):
-                xk = psum.tile([P, 512], F32, tag="xk")
-                transpose_head(nc, xk, words[:, 512 * h : 512 * h + 512], ident[:])
-                leave_bank(nc, gk_w[:, 512 * h : 512 * h + 512], xk)
-            gks[b] = gk
+        def copy_shared(m):
+            if m < NM:
+                sm = rawp.tile([P, 256], F32, tag="small")
+                nc.scalar.copy(
+                    out=sm[:].rearrange("p (r u) -> p r u", u=2),
+                    in_=shared[m][:].rearrange("p (u g r) -> p g r u", u=2, g=2)[:, 0],
+                )
+                small[m] = sm
 
-        def sums(s):
-            if 0 <= s < NF:
-                if not is_special(s):
-                    g_new = work.tile([P, 4 * D], BF16, tag="g", align_bytes=64)
-                    gts[s] = g_new
-                for h in range(H):
-                    if h == 1 and is_special(s):
-                        continue
-                    bank = xqs[(s, h)][:].bitcast(BF16).rearrange("p (u x e) -> p x u e", u=2, e=2)
-                    for side in range(2):
-                        i = 2 * (1 - side) + h
-                        o = D * (2 * side + h)
-                        nc.vector.tensor_tensor(
-                            out=gts[s][:, o : o + D].rearrange("p (x u e) -> p x u e", u=2, e=2),
-                            in0=bank,
-                            in1=bfull[:, D * i : D * i + D].rearrange("p (x u e) -> p x u e", u=2, e=2),
-                            op=ADD,
-                        )
-            for side, b in ((0, s), (1, s - TAIL)):
-                if NF <= b < B:
-                    g_tail = work.tile([P, 4 * D], BF16, tag="g", align_bytes=64)
-                    i = 2 * (1 - side)
-                    nc.vector.tensor_tensor(
-                        out=g_tail[:, 0 : H * D], in0=raws[b][:].bitcast(BF16), in1=bfull[:, D * i : D * i + H * D], op=ADD
-                    )
-                    gts[(side, b)] = g_tail
+        def turn_tail(m, pair):
+            if NM <= m < NG:
+                if pair == 0:
+                    raw = rawp.tile([P, GW // 2], F32, tag="raw")
+                    raws[m] = raw
+                xq = psum.tile([P, 512], F32, tag="xq")
+                transpose_pair(nc, xq, words_of(qts[m][:].bitcast(F32), pair), ident[:])
+                leave_bank(nc, words_of(raws[m][:], pair), xq)
 
-        def quantise_q(src, width):
-            cq = codes.tile([P, D], U32, tag="cq", align_bytes=64)
-            sq = codes.tile([P, D], U8, tag="sq", align_bytes=64)
-            nc.vector.quantize_mx(
-                out=cq[:, 0 : width // 4].bitcast(FP8X4), scales=sq[:, 0 : width // 4], in_=src[:, 0:width]
+        def turn_k(m, pairs):
+            if m < NG:
+                if 0 in pairs:
+                    gk = work.tile([P, GW], BF16, tag="gk", align_bytes=64)
+                    gks[m] = gk
+                for pair in pairs:
+                    xk = psum.tile([P, 512], F32, tag="xk")
+                    transpose_pair(nc, xk, words_of(kts[m][:].bitcast(F32), pair), ident[:])
+                    leave_bank(nc, words_of(gks[m][:].bitcast(F32), pair), xk)
+
+        def new_g(m):
+            g_new = work.tile([P, 2 * GW], BF16, tag="g", align_bytes=64)
+            gts[m] = g_new
+
+        def sums(m, pair):
+            bank = banks[(m, pair)][:].bitcast(BF16).rearrange("p (u x e) -> p x u e", u=2, e=2)
+            for side in range(2):
+                i = 2 * side + pair % 2
+                o = GW * side + D * pair
+                nc.vector.tensor_tensor(
+                    out=gts[m][:, o : o + D].rearrange("p (x u e) -> p x u e", u=2, e=2),
+                    in0=bank,
+                    in1=bfull[:, D * i : D * i + D].rearrange("p (x u e) -> p x u e", u=2, e=2),
+                    op=ADD,
+                )
+
+        def sums_tail(m, side):
+            o = GW * side
+            nc.vector.tensor_tensor(
+                out=gts[m][:, o : o + GW].rearrange("p (b x) -> p b x", b=2),
+                in0=raws[m][:].bitcast(BF16).rearrange("p (b x) -> p b x", b=2),
+                in1=bfull[:, 2 * D * side : 2 * D * side + 2 * D].unsqueeze(1).to_broadcast([P, 2, 2 * D]),
+                op=ADD,
             )
-            return cq, sq
 
-        def quantise_k(b):
-            ck = codes.tile([P, 512], U32, tag="ck", align_bytes=64)
-            sk = codes.tile([P, 512], U8, tag="sk", align_bytes=64)
-            nc.vector.quantize_mx(out=ck[:].bitcast(FP8X4), scales=sk[:], in_=gks[b][:])
-            cod[("k", b)] = (ck, sk, 0)
+        def sums_gpsimd(m):
+            for side in range(2):
+                o = GW * side + 3 * D
+                i = 2 * side + 1
+                nc.gpsimd.tensor_tensor(
+                    out=gts[m][:, o : o + 512],
+                    in0=small[m][:].bitcast(BF16),
+                    in1=bfull[:, D * i : D * i + 512],
+                    op=ADD,
+                )
 
-        def quants(j):
-            if 0 <= j < NF:
-                cq, sq = quantise_q(gts[j], 4 * D)
-                cod[("r", j)] = (cq, sq, 0)
-                cod[("w", j)] = (cq, sq, 512)
-                quantise_k(j)
-            if NF <= j < B:
-                cq, sq = quantise_q(gts[(0, j)], H * D)
-                cod[("r", j)] = (cq, sq, 0)
-            if NF <= j - TAIL < B:
-                cq, sq = quantise_q(gts[(1, j - TAIL)], H * D)
-                cod[("w", j - TAIL)] = (cq, sq, 0)
-                quantise_k(j - TAIL)
+        def sums_scalar(m, first, last):
+            bank = shared[m][:].bitcast(BF16).rearrange("p (c r e) -> p c r e", c=4, e=2)
+            for idx in range(first, last):
+                side = idx // 4
+                u = (idx // 2) % 2
+                e = idx % 2
+                col = 8 * (2 * side + 1) + 4 + 2 * u + e
+                o = GW * side + 3 * D + 512
+                nc.scalar.activation(
+                    out=gts[m][:, o : o + 512].rearrange("p (r j) -> p r j", j=4)[:, :, 2 * u + e],
+                    in_=bank[:, 2 * u + 1, :, e],
+                    func=IDENTITY,
+                    bias=b32[:, col : col + 1],
+                    scale=1.0,
+                )
 
-        def multiply(bank, b, left, right):
-            lc, ls, lb = left
-            mc, ms, mb = right
-            for h in range(H):
-                i = 2 * (b % 2) + h
+        def quantise(name, m, src):
+            cq = codes.tile([P, GW // 4], U32, tag="c" + name, align_bytes=64)
+            sq = codes.tile([P, GW // 4], U8, tag="s" + name, align_bytes=64)
+            nc.vector.quantize_mx(out=cq[:].bitcast(FP8X4), scales=sq[:], in_=src)
+            cod[(name, m)] = (cq, sq)
+
+        def quantise_side(m, side):
+            quantise("rw"[side], m, gts[m][:, GW * side : GW * side + GW])
+
+        def quantise_k(m):
+            quantise("k", m, gks[m][:])
+
+        def multiply(bank, left, right, shared_right):
+            lc, ls = left
+            mc, ms = right
+            for pair in range(GROUP):
                 for g in range(2):
-                    a = lb + 128 * (2 * h + g)
-                    m = mb + 128 * (2 * h + g)
+                    a = 128 * (2 * pair + g)
+                    b = 128 * (2 * (pair % 2) + g) if shared_right else a
                     nc.tensor.matmul_mx(
-                        out=bank[:, 128 * i : 128 * i + 128],
+                        out=bank[:, 128 * pair : 128 * pair + 128],
                         lhsT=lc[:, a : a + 128].bitcast(FP8X4),
                         lhsT_scale=ls[:, a : a + 128],
-                        rhs=mc[:, m : m + 128].bitcast(FP8X4),
-                        rhs_scale=ms[:, m : m + 128],
+                        rhs=mc[:, b : b + 128].bitcast(FP8X4),
+                        rhs_scale=ms[:, b : b + 128],
                         start=(g == 0),
                         stop=(g == 1),
                     )
 
-        def mult_rel(b):
-            if 0 <= b < B:
-                if b % 2 == 0:
-                    rel_new = psum.tile([P, 512], F32, tag="rel", bufs=1)
-                    rels[b // 2] = rel_new
-                multiply(rels[b // 2], b, cod[("r", b)], cod[("e", 0)])
+        def mult_rel(m):
+            rel = psum.tile([P, 512], F32, tag="rel", bufs=1)
+            multiply(rel, cod[("r", m)], (rc, rs), True)
+            rels[m] = rel
 
-        def mult_content(gi):
+        def mult_content(m):
             cont = psum.tile([P, 512], F32, tag="cont", bufs=1)
-            for b in (2 * gi, 2 * gi + 1):
-                multiply(cont, b, cod[("w", b)], cod[("k", b)])
-            conts[gi] = cont
+            multiply(cont, cod[("w", m)], cod[("k", m)], False)
+            conts[m] = cont
 
-        def offload(s):
-            for b in range(s + 1, s + PERIOD + 1):
-                if is_special(b):
-                    part = s - (b - PERIOD)
-                    bank = xss[b][:].bitcast(BF16).rearrange("p (c r e) -> p c r e", c=4, e=2)
-                    for idx in range(16 * part // PERIOD, 16 * (part + 1) // PERIOD):
-                        side = idx // 8
-                        g = (idx // 4) % 2
-                        u = (idx // 2) % 2
-                        e = idx % 2
-                        col = 8 * (2 * (1 - side) + 1) + 4 * g + 2 * u + e
-                        o = D * (2 * side + 1) + 512 * g
-                        nc.scalar.activation(
-                            out=gts[b][:, o : o + 512].rearrange("p (r j) -> p r j", j=4)[:, :, 2 * u + e],
-                            in_=bank[:, 2 * u + g, :, e],
-                            func=IDENTITY,
-                            bias=b32[:, col : col + 1],
-                            scale=1.0,
-                        )
-
-        def area_of(gi):
-            base = min(GROUP * SLOT * gi, B * H * T * T - GROUP * SLOT)
+        def area_of(m):
+            base = min(GROUP * SLOT * m, B * H * T * T - GROUP * SLOT)
             return out_flat[base : base + GROUP * SLOT]
 
-        def pad_rel(gi):
+        def pad_rel(m):
             nc.scalar.copy(
-                out=stg[gi % NSTG][:].rearrange("p (i c) -> p i c", i=GROUP)[:, :, 1 : T + 1],
-                in_=rels[gi][:].rearrange("p (i j) -> p i j", i=GROUP),
+                out=stg[m % NSTG][:].rearrange("p (i c) -> p i c", i=GROUP)[:, :, 1 : T + 1],
+                in_=rels[m][:].rearrange("p (i j) -> p i j", i=GROUP),
             )
 
-        def park(gi):
+        def move_content(m):
+            cs = back_pool.tile([P, GROUP * T], F32, tag="cs")
+            nc.scalar.copy(out=cs[:], in_=conts[m][:])
+            css[m] = cs
+
+        def park(m):
             nc.sync.dma_start(
-                out=area_of(gi).rearrange("(i t c) -> t i c", i=GROUP, t=T),
-                in_=stg[gi % NSTG][:].rearrange("p (i c) -> p i c", i=GROUP),
+                out=area_of(m).rearrange("(i t c) -> t i c", i=GROUP, t=T),
+                in_=stg[m % NSTG][:].rearrange("p (i c) -> p i c", i=GROUP),
             )
 
-        def fetch(gi):
+        def fetch(m):
             rb = back_pool.tile([P, GROUP * T], F32, tag="rb")
             nc.sync.dma_start(
                 out=rb[:].rearrange("p (i j) -> p i j", i=GROUP),
-                in_=area_of(gi).rearrange("(i f) -> i f", i=GROUP)[:, T:SLOT].rearrange("i (t j) -> t i j", t=T),
+                in_=area_of(m).rearrange("(i f) -> i f", i=GROUP)[:, T:SLOT].rearrange("i (t j) -> t i j", t=T),
             )
-            rbs[gi] = rb
+            rbs[m] = rb
 
-        def move_content(gi):
-            cs = back_pool.tile([P, GROUP * T], F32, tag="cs")
-            nc.scalar.copy(out=cs[:], in_=conts[gi][:])
-            css[gi] = cs
-
-        def final_add(gi):
+        def final_add(m, engine, first):
             fin = back_pool.tile([P, GROUP * T], F32, tag="fin")
-            if on_gpsimd(gi):
-                nc.gpsimd.tensor_tensor(out=fin[:], in0=css[gi][:], in1=rbs[gi][:], op=ADD)
-            else:
-                nc.vector.tensor_tensor(out=fin[:], in0=conts[gi][:], in1=rbs[gi][:], op=ADD)
-            fins[gi] = fin
+            engine.tensor_tensor(out=fin[:], in0=first, in1=rbs[m][:], op=ADD)
+            fins[m] = fin
 
-        def final_store(gi):
+        def final_store(m):
             nc.sync.dma_start(
-                out=out[2 * gi : 2 * gi + 2].rearrange("b h t j -> t (b h) j"),
-                in_=fins[gi][:].rearrange("p (i j) -> p i j", i=GROUP),
+                out=out[2 * m : 2 * m + 2].rearrange("b h t j -> t (b h) j"),
+                in_=fins[m][:].rearrange("p (i j) -> p i j", i=GROUP),
             )
 
-        groups = range(NGROUPS)
-        for s in range(-1, fa_step(NGROUPS - 1) + 1):
-            load_q(s + 1 + PF)
-            for b in range(PF, B):
-                if c_step(b) == s + 1 + PF:
-                    load_k(b)
-            load_q_special(s + PERIOD + PF)
-            due = [gi for gi in groups if fa_step(gi) == s]
-            padded = [gi for gi in groups if 2 * gi + 3 == s]
-            early = [gi for gi in groups if on_gpsimd(gi) and 2 * gi + 4 == s]
-            for gi in early + [gi for gi in due if not on_gpsimd(gi)]:
-                mult_content(gi)
-            for gi in padded:
-                pad_rel(gi)
-            next_k = [b for b in range(B) if c_step(b) == s + 1]
-            if s >= 0:
-                for b in next_k:
-                    turn_k(b)
-            for gi in early:
-                move_content(gi)
-            turn_special(s + PERIOD)
-            sums(s)
-            turn_q(s + 1)
-            if s == -1:
-                for b in next_k:
-                    turn_k(b)
-                prepare_r_tensor()
-            if s == 1:
+        turn_q(0, 0)
+        turn_q(0, 1)
+        turn_shared(0)
+        copy_shared(0)
+
+        for m in range(NM):
+            if m > 0:
+                load_q(m - 1 + PF)
+                load_k(m - 1 + PF)
+            new_g(m)
+            if m >= 2:
+                mult_rel(m - 2)
+                mult_content(m - 2)
+            sums(m, 0)
+            sums_gpsimd(m)
+            sums_scalar(m, 0, 2)
+            if m >= 2:
+                pad_rel(m - 2)
+                move_content(m - 2)
+            turn_q(m, 2)
+            turn_shared(m + 1)
+            copy_shared(m + 1)
+            turn_tail(m + 1, 0)
+            sums(m, 1)
+            turn_k(m, (0, 1))
+            sums_scalar(m, 2, 5)
+            turn_q(m + 1, 0)
+            turn_tail(m + 1, 1)
+            sums(m, 2)
+            turn_k(m, (2, 3))
+            turn_q(m + 1, 1)
+            turn_tail(m + 1, 2)
+            turn_tail(m + 1, 3)
+            sums_scalar(m, 5, 8)
+            if m == 0:
+                prepare_r()
+            if m == 1:
                 nc.vector.quantize_mx(out=rc[:].bitcast(FP8X4), scales=rs[:], in_=gr[:])
-            quants(s - 1)
-            mult_rel(s - 1)
-            offload(s)
-            for gi in due:
-                final_add(gi)
-            for gi in groups:
-                if 2 * gi + 4 == s:
-                    fetch(gi)
-            for gi in padded:
-                park(gi)
-            for gi in due:
-                final_store(gi)
+            if m >= 1:
+                quantise_side(m - 1, 0)
+                quantise_side(m - 1, 1)
+                quantise_k(m - 1)
+            if m >= 4:
+                final_add(m - 4, nc.gpsimd, css[m - 4][:])
+            if m >= 3:
+                fetch(m - 3)
+            if m >= 2:
+                park(m - 2)
+            if m >= 5:
+                final_store(m - 5)
+
+        y, z = NM, NM + 1
+        load_q(NM - 1 + PF)
+        new_g(y)
+        mult_rel(NM - 2)
+        mult_content(NM - 2)
+        sums_tail(y, 0)
+        pad_rel(NM - 2)
+        move_content(NM - 2)
+        for pair in range(GROUP):
+            turn_tail(z, pair)
+        turn_k(y, (0, 1, 2, 3))
+        quantise_side(NM - 1, 0)
+        quantise_side(NM - 1, 1)
+        quantise_k(NM - 1)
+        final_add(NM - 4, nc.gpsimd, css[NM - 4][:])
+        fetch(NM - 3)
+        park(NM - 2)
+        final_store(NM - 5)
+
+        new_g(z)
+        mult_rel(NM - 1)
+        mult_content(NM - 1)
+        sums_tail(z, 0)
+        pad_rel(NM - 1)
+        move_content(NM - 1)
+        turn_k(z, (0, 1, 2, 3))
+        quantise_side(y, 0)
+        mult_rel(y)
+        pad_rel(y)
+        fetch(NM - 2)
+        park(NM - 1)
+        final_store(NM - 4)
+        final_add(NM - 3, nc.gpsimd, css[NM - 3][:])
+        final_store(NM - 3)
+        park(y)
+        fetch(NM - 1)
+        sums_tail(y, 1)
+        quantise_side(z, 0)
+        mult_rel(z)
+        pad_rel(z)
+        final_add(NM - 2, nc.gpsimd, css[NM - 2][:])
+        final_store(NM - 2)
+        fetch(y)
+        park(z)
+        sums_tail(z, 1)
+        final_add(NM - 1, nc.gpsimd, css[NM - 1][:])
+        final_store(NM - 1)
+        fetch(z)
+        quantise_side(y, 1)
+        quantise_k(y)
+        quantise_side(z, 1)
+        mult_content(y)
+        quantise_k(z)
+        final_add(y, nc.vector, conts[y][:])
+        final_store(y)
+        mult_content(z)
+        final_add(z, nc.vector, conts[z][:])
+        final_store(z)

@@ -17,7 +17,7 @@ FLOPS = 2 * 2 * B * H * T * T * D
 
 GROUP = 4
 NG = B * H // GROUP
-NM = NG - 2
+NM = NG - 1
 SLOT = (T + 1) * T
 NSTG = 3
 PF = 3
@@ -52,7 +52,7 @@ def tile_relativepositionembedding_pa_t_kernel(tc, q, k, r_w_bias, r_r_bias, rel
         io = ctx.enter_context(tc.tile_pool(name="io", bufs=PF + 1))
         rawp = ctx.enter_context(tc.tile_pool(name="rawp", bufs=2))
         work = ctx.enter_context(tc.tile_pool(name="work", bufs=2))
-        codes = ctx.enter_context(tc.tile_pool(name="codes", bufs=3))
+        codes = ctx.enter_context(tc.tile_pool(name="codes", bufs=4))
         back_pool = ctx.enter_context(tc.tile_pool(name="backp", bufs=3))
         psum = ctx.enter_context(tc.psum_pool(name="psum", bufs=2))
         ctx.enter_context(tc.manual_schedule())
@@ -92,12 +92,15 @@ def tile_relativepositionembedding_pa_t_kernel(tc, q, k, r_w_bias, r_r_bias, rel
         nc.sync.dma_start(out=qts[0][:, D : 2 * D], in_=q[0][:, 1, :])
         nc.sync.dma_start(out=qts[0][:, 2 * D : 4 * D], in_=q[1].rearrange("t h d -> t (h d)"))
         load_q(1)
-        load_k(0)
         rsb = const.tile([P, H * D], BF16)
         nc.sync.dma_start(out=rsb[:], in_=rel_pos_emb.rearrange("j h d -> j (h d)"))
+        load_k(0)
         load_k(1)
         load_q(2)
         load_k(2)
+
+        def offloaded(m):
+            return m < NM - 1
 
         stg = []
         for s in range(NSTG):
@@ -152,24 +155,24 @@ def tile_relativepositionembedding_pa_t_kernel(tc, q, k, r_w_bias, r_r_bias, rel
         cod = {}
         rels = {}
         conts = {}
-        css = {}
         rbs = {}
         fins = {}
 
         def turn_q(m, pair):
             if m < NM:
-                xq = psum.tile([P, 512], F32, tag="xq")
+                xq = psum.tile([P, 512], F32, tag="xq", bufs=3)
                 transpose_pair(nc, xq, words_of(qts[m][:].bitcast(F32), pair), ident[:])
                 banks[(m, pair)] = xq
 
         def turn_shared(m):
             if m < NM:
-                xs = psum.tile([P, 512], F32, tag="xs")
+                xs = psum.tile([P, 512], F32, tag="xs", bufs=1)
                 transpose_pair(nc, xs, words_of(qts[m][:].bitcast(F32), 3), ident[:])
                 shared[m] = xs
+                banks[(m, 3)] = xs
 
         def copy_shared(m):
-            if m < NM:
+            if offloaded(m):
                 sm = rawp.tile([P, 256], F32, tag="small")
                 nc.scalar.copy(
                     out=sm[:].rearrange("p (r u) -> p r u", u=2),
@@ -182,7 +185,7 @@ def tile_relativepositionembedding_pa_t_kernel(tc, q, k, r_w_bias, r_r_bias, rel
                 if pair == 0:
                     raw = rawp.tile([P, GW // 2], F32, tag="raw")
                     raws[m] = raw
-                xq = psum.tile([P, 512], F32, tag="xq")
+                xq = psum.tile([P, 512], F32, tag="xq", bufs=3)
                 transpose_pair(nc, xq, words_of(qts[m][:].bitcast(F32), pair), ident[:])
                 leave_bank(nc, words_of(raws[m][:], pair), xq)
 
@@ -222,7 +225,7 @@ def tile_relativepositionembedding_pa_t_kernel(tc, q, k, r_w_bias, r_r_bias, rel
             )
 
         def sums_gpsimd(m):
-            for side in range(2):
+            for side in (1, 0):
                 o = GW * side + 3 * D
                 i = 2 * side + 1
                 nc.gpsimd.tensor_tensor(
@@ -282,13 +285,13 @@ def tile_relativepositionembedding_pa_t_kernel(tc, q, k, r_w_bias, r_r_bias, rel
             multiply(rel, cod[("r", m)], (rc, rs), True)
             rels[m] = rel
 
-        def mult_content(m):
-            cont = psum.tile([P, 512], F32, tag="cont", bufs=1)
+        def mult_content(m, tag="cont"):
+            cont = psum.tile([P, 512], F32, tag=tag, bufs=1)
             multiply(cont, cod[("w", m)], cod[("k", m)], False)
             conts[m] = cont
 
         def area_of(m):
-            base = min(GROUP * SLOT * m, B * H * T * T - GROUP * SLOT)
+            base = max(B * H * T * T - GROUP * SLOT * (NG - m), 0)
             return out_flat[base : base + GROUP * SLOT]
 
         def pad_rel(m):
@@ -296,11 +299,6 @@ def tile_relativepositionembedding_pa_t_kernel(tc, q, k, r_w_bias, r_r_bias, rel
                 out=stg[m % NSTG][:].rearrange("p (i c) -> p i c", i=GROUP)[:, :, 1 : T + 1],
                 in_=rels[m][:].rearrange("p (i j) -> p i j", i=GROUP),
             )
-
-        def move_content(m):
-            cs = back_pool.tile([P, GROUP * T], F32, tag="cs")
-            nc.scalar.copy(out=cs[:], in_=conts[m][:])
-            css[m] = cs
 
         def park(m):
             nc.sync.dma_start(
@@ -316,9 +314,9 @@ def tile_relativepositionembedding_pa_t_kernel(tc, q, k, r_w_bias, r_r_bias, rel
             )
             rbs[m] = rb
 
-        def final_add(m, engine, first):
+        def final_add(m):
             fin = back_pool.tile([P, GROUP * T], F32, tag="fin")
-            engine.tensor_tensor(out=fin[:], in0=first, in1=rbs[m][:], op=ADD)
+            nc.vector.tensor_tensor(out=fin[:], in0=conts[m][:], in1=rbs[m][:], op=ADD)
             fins[m] = fin
 
         def final_store(m):
@@ -327,8 +325,8 @@ def tile_relativepositionembedding_pa_t_kernel(tc, q, k, r_w_bias, r_r_bias, rel
                 in_=fins[m][:].rearrange("p (i j) -> p i j", i=GROUP),
             )
 
-        turn_q(0, 0)
-        turn_q(0, 1)
+        for pair in range(3):
+            turn_q(0, pair)
         turn_shared(0)
         copy_shared(0)
 
@@ -336,103 +334,92 @@ def tile_relativepositionembedding_pa_t_kernel(tc, q, k, r_w_bias, r_r_bias, rel
             if m > 0:
                 load_q(m - 1 + PF)
                 load_k(m - 1 + PF)
+            if m >= 3:
+                fetch(m - 3)
+            if m >= 5:
+                final_store(m - 5)
             new_g(m)
             if m >= 2:
                 mult_rel(m - 2)
-                mult_content(m - 2)
             sums(m, 0)
-            sums_gpsimd(m)
-            sums_scalar(m, 0, 2)
+            if offloaded(m):
+                sums_gpsimd(m)
+                sums_scalar(m, 0, 2)
             if m >= 2:
                 pad_rel(m - 2)
-                move_content(m - 2)
-            turn_q(m, 2)
-            turn_shared(m + 1)
-            copy_shared(m + 1)
-            turn_tail(m + 1, 0)
-            sums(m, 1)
-            turn_k(m, (0, 1))
-            sums_scalar(m, 2, 5)
+                park(m - 2)
             turn_q(m + 1, 0)
+            turn_tail(m + 1, 0)
+            if offloaded(m):
+                sums_scalar(m, 2, 8)
+            if m > 0:
+                turn_k(m, (0,))
+            sums(m, 1)
+            turn_q(m + 1, 1)
             turn_tail(m + 1, 1)
             sums(m, 2)
-            turn_k(m, (2, 3))
-            turn_q(m + 1, 1)
+            turn_q(m + 1, 2)
             turn_tail(m + 1, 2)
+            if not offloaded(m):
+                sums(m, 3)
+            if m >= 4:
+                final_add(m - 4)
+            if m >= 3:
+                mult_content(m - 3)
+            turn_shared(m + 1)
+            copy_shared(m + 1)
             turn_tail(m + 1, 3)
-            sums_scalar(m, 5, 8)
-            if m == 0:
+            if m > 0:
+                turn_k(m, (1, 2, 3))
+            else:
                 prepare_r()
+                turn_k(m, (0, 1, 2, 3))
             if m == 1:
+                quantise_side(0, 0)
+                quantise_side(0, 1)
                 nc.vector.quantize_mx(out=rc[:].bitcast(FP8X4), scales=rs[:], in_=gr[:])
-            if m >= 1:
+                quantise_k(0)
+            if m >= 2:
+                quantise_k(m - 1)
                 quantise_side(m - 1, 0)
                 quantise_side(m - 1, 1)
-                quantise_k(m - 1)
-            if m >= 4:
-                final_add(m - 4, nc.gpsimd, css[m - 4][:])
-            if m >= 3:
-                fetch(m - 3)
-            if m >= 2:
-                park(m - 2)
-            if m >= 5:
-                final_store(m - 5)
 
-        y, z = NM, NM + 1
-        load_q(NM - 1 + PF)
-        new_g(y)
-        mult_rel(NM - 2)
-        mult_content(NM - 2)
-        sums_tail(y, 0)
-        pad_rel(NM - 2)
-        move_content(NM - 2)
-        for pair in range(GROUP):
-            turn_tail(z, pair)
-        turn_k(y, (0, 1, 2, 3))
-        quantise_side(NM - 1, 0)
-        quantise_side(NM - 1, 1)
-        quantise_k(NM - 1)
-        final_add(NM - 4, nc.gpsimd, css[NM - 4][:])
+        y, z = NM - 1, NM
         fetch(NM - 3)
-        park(NM - 2)
         final_store(NM - 5)
-
         new_g(z)
-        mult_rel(NM - 1)
-        mult_content(NM - 1)
+        mult_rel(NM - 2)
+        pad_rel(NM - 2)
+        park(NM - 2)
         sums_tail(z, 0)
-        pad_rel(NM - 1)
-        move_content(NM - 1)
-        turn_k(z, (0, 1, 2, 3))
+        final_add(NM - 4)
+        mult_content(NM - 3)
         quantise_side(y, 0)
         mult_rel(y)
         pad_rel(y)
-        fetch(NM - 2)
-        park(NM - 1)
-        final_store(NM - 4)
-        final_add(NM - 3, nc.gpsimd, css[NM - 3][:])
-        final_store(NM - 3)
         park(y)
-        fetch(NM - 1)
-        sums_tail(y, 1)
         quantise_side(z, 0)
         mult_rel(z)
         pad_rel(z)
-        final_add(NM - 2, nc.gpsimd, css[NM - 2][:])
-        final_store(NM - 2)
-        fetch(y)
+        fetch(NM - 2)
         park(z)
-        sums_tail(z, 1)
-        final_add(NM - 1, nc.gpsimd, css[NM - 1][:])
-        final_store(NM - 1)
-        fetch(z)
-        quantise_side(y, 1)
+        turn_k(z, (0, 1, 2, 3))
+        final_store(NM - 4)
+        final_add(NM - 3)
+        mult_content(NM - 2)
         quantise_k(y)
-        quantise_side(z, 1)
+        quantise_side(y, 1)
+        fetch(y)
+        final_store(NM - 3)
+        sums_tail(z, 1)
+        final_add(NM - 2)
         mult_content(y)
+        fetch(z)
+        final_store(NM - 2)
         quantise_k(z)
-        final_add(y, nc.vector, conts[y][:])
+        quantise_side(z, 1)
+        mult_content(z, "xs")
+        final_add(y)
         final_store(y)
-        mult_content(z)
-        final_add(z, nc.vector, conts[z][:])
+        final_add(z)
         final_store(z)

@@ -100,7 +100,7 @@ def tile_relativepositionembedding_pa_t_kernel(tc, q, k, r_w_bias, r_r_bias, rel
         load_k(2)
 
         def offloaded(m):
-            return m < NM - 1
+            return 2 <= m < NM - 1
 
         stg = []
         for s in range(NSTG):
@@ -189,15 +189,18 @@ def tile_relativepositionembedding_pa_t_kernel(tc, q, k, r_w_bias, r_r_bias, rel
                 transpose_pair(nc, xq, words_of(qts[m][:].bitcast(F32), pair), ident[:])
                 leave_bank(nc, words_of(raws[m][:], pair), xq)
 
-        def turn_k(m, pairs):
-            if m < NG:
-                if 0 in pairs:
-                    gk = work.tile([P, GW], BF16, tag="gk", align_bytes=64)
-                    gks[m] = gk
-                for pair in pairs:
-                    xk = psum.tile([P, 512], F32, tag="xk")
-                    transpose_pair(nc, xk, words_of(kts[m][:].bitcast(F32), pair), ident[:])
-                    leave_bank(nc, words_of(gks[m][:].bitcast(F32), pair), xk)
+        def turn_k(m, *pairs):
+            for pair in pairs:
+                xk = psum.tile([P, 512], F32, tag="xk")
+                transpose_pair(nc, xk, words_of(kts[m][:].bitcast(F32), pair), ident[:])
+                banks[("k", m, pair)] = xk
+
+        def copy_k(m, *pairs):
+            if 0 in pairs:
+                gk = work.tile([P, GW], BF16, tag="gk", align_bytes=64)
+                gks[m] = gk
+            for pair in pairs:
+                leave_bank(nc, words_of(gks[m][:].bitcast(F32), pair), banks[("k", m, pair)])
 
         def new_g(m):
             g_new = work.tile([P, 2 * GW], BF16, tag="g", align_bytes=64)
@@ -339,24 +342,24 @@ def tile_relativepositionembedding_pa_t_kernel(tc, q, k, r_w_bias, r_r_bias, rel
             if m >= 5:
                 final_store(m - 5)
             new_g(m)
+            if m >= 1:
+                copy_k(m, 0, 1)
             if m >= 2:
                 mult_rel(m - 2)
             sums(m, 0)
             if offloaded(m):
                 sums_gpsimd(m)
-                sums_scalar(m, 0, 2)
-            if m >= 2:
-                pad_rel(m - 2)
-                park(m - 2)
             turn_q(m + 1, 0)
             turn_tail(m + 1, 0)
             if offloaded(m):
-                sums_scalar(m, 2, 8)
-            if m > 0:
-                turn_k(m, (0,))
+                sums_scalar(m, 0, 8)
+            if m >= 1:
+                turn_k(m, 2)
             sums(m, 1)
             turn_q(m + 1, 1)
             turn_tail(m + 1, 1)
+            if m >= 1:
+                turn_k(m, 3)
             sums(m, 2)
             turn_q(m + 1, 2)
             turn_tail(m + 1, 2)
@@ -366,14 +369,20 @@ def tile_relativepositionembedding_pa_t_kernel(tc, q, k, r_w_bias, r_r_bias, rel
                 final_add(m - 4)
             if m >= 3:
                 mult_content(m - 3)
+            if m >= 1:
+                copy_k(m, 2, 3)
+            if m >= 2:
+                pad_rel(m - 2)
+                park(m - 2)
             turn_shared(m + 1)
             copy_shared(m + 1)
             turn_tail(m + 1, 3)
-            if m > 0:
-                turn_k(m, (1, 2, 3))
-            else:
+            if m == 0:
                 prepare_r()
-                turn_k(m, (0, 1, 2, 3))
+                for pair in range(GROUP):
+                    turn_k(0, pair)
+                    copy_k(0, pair)
+            turn_k(m + 1, 0, 1)
             if m == 1:
                 quantise_side(0, 0)
                 quantise_side(0, 1)
@@ -388,13 +397,16 @@ def tile_relativepositionembedding_pa_t_kernel(tc, q, k, r_w_bias, r_r_bias, rel
         fetch(NM - 3)
         final_store(NM - 5)
         new_g(z)
+        copy_k(z, 0, 1)
         mult_rel(NM - 2)
         pad_rel(NM - 2)
         park(NM - 2)
         sums_tail(z, 0)
+        turn_k(z, 2, 3)
         final_add(NM - 4)
         mult_content(NM - 3)
         quantise_side(y, 0)
+        copy_k(z, 2, 3)
         mult_rel(y)
         pad_rel(y)
         park(y)
@@ -403,7 +415,6 @@ def tile_relativepositionembedding_pa_t_kernel(tc, q, k, r_w_bias, r_r_bias, rel
         pad_rel(z)
         fetch(NM - 2)
         park(z)
-        turn_k(z, (0, 1, 2, 3))
         final_store(NM - 4)
         final_add(NM - 3)
         mult_content(NM - 2)

@@ -299,27 +299,26 @@ def tile_relativepositionembedding_pa_t_kernel(tc, q, k, r_w_bias, r_r_bias, rel
 
         def pad_rel(m):
             nc.scalar.copy(
-                out=stg[m % NSTG][:].rearrange("p (i c) -> p i c", i=GROUP)[:, :, 1 : T + 1],
-                in_=rels[m][:].rearrange("p (i j) -> p i j", i=GROUP),
+                out=stg[m % NSTG][:, GROUP:].rearrange("p (j i) -> p j i", i=GROUP),
+                in_=rels[m][:].rearrange("p (i j) -> p j i", i=GROUP),
             )
 
         def park(m):
-            nc.sync.dma_start(
-                out=area_of(m).rearrange("(i t c) -> t i c", i=GROUP, t=T),
-                in_=stg[m % NSTG][:].rearrange("p (i c) -> p i c", i=GROUP),
-            )
+            nc.sync.dma_start(out=area_of(m).rearrange("(t x) -> t x", t=T), in_=stg[m % NSTG][:])
 
         def fetch(m):
             rb = back_pool.tile([P, GROUP * T], F32, tag="rb")
-            nc.sync.dma_start(
-                out=rb[:].rearrange("p (i j) -> p i j", i=GROUP),
-                in_=area_of(m).rearrange("(i f) -> i f", i=GROUP)[:, T:SLOT].rearrange("i (t j) -> t i j", t=T),
-            )
+            nc.sync.dma_start(out=rb[:], in_=area_of(m)[GROUP * T :].rearrange("(t x) -> t x", t=T))
             rbs[m] = rb
 
         def final_add(m):
             fin = back_pool.tile([P, GROUP * T], F32, tag="fin")
-            nc.vector.tensor_tensor(out=fin[:], in0=conts[m][:], in1=rbs[m][:], op=ADD)
+            nc.vector.tensor_tensor(
+                out=fin[:].rearrange("p (i j) -> p j i", i=GROUP),
+                in0=conts[m][:].rearrange("p (i j) -> p j i", i=GROUP),
+                in1=rbs[m][:].rearrange("p (j i) -> p j i", i=GROUP),
+                op=ADD,
+            )
             fins[m] = fin
 
         def final_store(m):

@@ -304,7 +304,7 @@ def tile_relativepositionembedding_pa_t_kernel(tc, q, k, r_w_bias, r_r_bias, rel
             )
 
         def park(m):
-            nc.sync.dma_start(out=area_of(m).rearrange("(t x) -> t x", t=T), in_=stg[m % NSTG][:])
+            nc.scalar.dma_start(out=area_of(m).rearrange("(t x) -> t x", t=T), in_=stg[m % NSTG][:])
 
         def fetch(m):
             rb = back_pool.tile([P, GROUP * T], F32, tag="rb")
@@ -321,8 +321,8 @@ def tile_relativepositionembedding_pa_t_kernel(tc, q, k, r_w_bias, r_r_bias, rel
             )
             fins[m] = fin
 
-        def final_store(m):
-            nc.sync.dma_start(
+        def final_store(m, queue):
+            queue.dma_start(
                 out=out[2 * m : 2 * m + 2].rearrange("b h t j -> t (b h) j"),
                 in_=fins[m][:].rearrange("p (i j) -> p i j", i=GROUP),
             )
@@ -338,8 +338,6 @@ def tile_relativepositionembedding_pa_t_kernel(tc, q, k, r_w_bias, r_r_bias, rel
                 load_k(m - 1 + PF)
             if m >= 3:
                 fetch(m - 3)
-            if m >= 5:
-                final_store(m - 5)
             new_g(m)
             if m >= 1:
                 copy_k(m, 0, 1)
@@ -370,6 +368,8 @@ def tile_relativepositionembedding_pa_t_kernel(tc, q, k, r_w_bias, r_r_bias, rel
                 mult_content(m - 3)
             if m >= 1:
                 copy_k(m, 2, 3)
+            if m >= 5:
+                final_store(m - 5, nc.scalar)
             if m >= 2:
                 pad_rel(m - 2)
                 park(m - 2)
@@ -394,7 +394,7 @@ def tile_relativepositionembedding_pa_t_kernel(tc, q, k, r_w_bias, r_r_bias, rel
 
         y, z = NM - 1, NM
         fetch(NM - 3)
-        final_store(NM - 5)
+        final_store(NM - 5, nc.sync)
         new_g(z)
         copy_k(z, 0, 1)
         mult_rel(NM - 2)
@@ -414,22 +414,22 @@ def tile_relativepositionembedding_pa_t_kernel(tc, q, k, r_w_bias, r_r_bias, rel
         pad_rel(z)
         fetch(NM - 2)
         park(z)
-        final_store(NM - 4)
+        final_store(NM - 4, nc.sync)
         final_add(NM - 3)
         mult_content(NM - 2)
         quantise_k(y)
         quantise_side(y, 1)
         fetch(y)
-        final_store(NM - 3)
+        final_store(NM - 3, nc.sync)
         sums_tail(z, 1)
         final_add(NM - 2)
         mult_content(y)
         fetch(z)
-        final_store(NM - 2)
+        final_store(NM - 2, nc.sync)
         quantise_k(z)
         quantise_side(z, 1)
         mult_content(z, "xs")
         final_add(y)
-        final_store(y)
+        final_store(y, nc.sync)
         final_add(z)
-        final_store(z)
+        final_store(z, nc.sync)

@@ -57,6 +57,8 @@ def tile_relativepositionembedding_pa_t_kernel(tc, q, k, r_w_bias, r_r_bias, rel
         psum = ctx.enter_context(tc.psum_pool(name="psum", bufs=2))
         ctx.enter_context(tc.manual_schedule())
 
+        brow = const.tile([P, D], BF16)
+        nc.gpsimd.memset(brow[:].bitcast(F32), 0.0)
         ident = const.tile([P, P], F32)
         make_identity(nc, ident[:])
 
@@ -82,13 +84,10 @@ def tile_relativepositionembedding_pa_t_kernel(tc, q, k, r_w_bias, r_r_bias, rel
                 )
                 kts[m] = kt
 
-        brow = const.tile([P, D], BF16)
-        nc.vector.memset(brow[:].bitcast(F32), 0.0)
-
         load_q(0, pieces=2)
-        nc.sync.dma_start(out=qts[0][:, 0:D], in_=q[0][:, 0, :])
         nc.sync.dma_start(out=brow[0:2, :], in_=r_r_bias)
         nc.sync.dma_start(out=brow[2:4, :], in_=r_w_bias)
+        nc.sync.dma_start(out=qts[0][:, 0:D], in_=q[0][:, 0, :])
         nc.sync.dma_start(out=qts[0][:, D : 2 * D], in_=q[0][:, 1, :])
         nc.sync.dma_start(out=qts[0][:, 2 * D : 4 * D], in_=q[1].rearrange("t h d -> t (h d)"))
         load_q(1)
@@ -99,8 +98,11 @@ def tile_relativepositionembedding_pa_t_kernel(tc, q, k, r_w_bias, r_r_bias, rel
         load_q(2)
         load_k(2)
 
-        def offloaded(m):
-            return 2 <= m < NM - 1
+        def with_gpsimd(m):
+            return 1 <= m < NM
+
+        def with_scalar(m):
+            return 3 <= m < NM - 1
 
         stg = []
         for s in range(NSTG):
@@ -117,8 +119,8 @@ def tile_relativepositionembedding_pa_t_kernel(tc, q, k, r_w_bias, r_r_bias, rel
             )
         bsm = const.tile([P, 16], F32)
         nc.vector.tensor_copy(
-            out=bsm[:].rearrange("p (i c) -> p i c", c=4),
-            in_=pb[:].rearrange("p (c i) -> p i c", c=4)[:, 0:4, :],
+            out=bsm[:].rearrange("p (h s c) -> p s h c", s=2, c=4),
+            in_=pb[:].rearrange("p (c i) -> p i c", c=4)[:, 0:4, :].rearrange("p (s h) c -> p s h c", s=2),
         )
         bfull = const.tile([P, 4 * D], BF16, align_bytes=64)
         bfull_w = bfull[:].bitcast(F32)
@@ -129,10 +131,8 @@ def tile_relativepositionembedding_pa_t_kernel(tc, q, k, r_w_bias, r_r_bias, rel
                 in_=bsm[:, 4 * i : 4 * i + 4].rearrange("p (g u) -> p g u", g=2).unsqueeze(2).to_broadcast([P, 2, T, 2]),
             )
 
-        widen(nc.vector.tensor_copy, 0)
-        widen(nc.scalar.copy, 2)
-        widen(nc.vector.tensor_copy, 1)
-        widen(nc.scalar.copy, 3)
+        for i in range(4):
+            widen(nc.scalar.copy, i)
         b32 = const.tile([P, 32], F32)
         nc.vector.tensor_copy(out=b32[:], in_=bsm[:].bitcast(BF16))
 
@@ -172,7 +172,7 @@ def tile_relativepositionembedding_pa_t_kernel(tc, q, k, r_w_bias, r_r_bias, rel
                 banks[(m, 3)] = xs
 
         def copy_shared(m):
-            if offloaded(m):
+            if with_gpsimd(m):
                 sm = rawp.tile([P, 256], F32, tag="small")
                 nc.scalar.copy(
                     out=sm[:].rearrange("p (r u) -> p r u", u=2),
@@ -197,7 +197,7 @@ def tile_relativepositionembedding_pa_t_kernel(tc, q, k, r_w_bias, r_r_bias, rel
 
         def copy_k(m, *pairs):
             if 0 in pairs:
-                gk = work.tile([P, GW], BF16, tag="gk", align_bytes=64)
+                gk = work.tile([P, GW], BF16, tag="gk", bufs=3, align_bytes=64)
                 gks[m] = gk
             for pair in pairs:
                 leave_bank(nc, words_of(gks[m][:].bitcast(F32), pair), banks[("k", m, pair)])
@@ -206,92 +206,117 @@ def tile_relativepositionembedding_pa_t_kernel(tc, q, k, r_w_bias, r_r_bias, rel
             g_new = work.tile([P, 2 * GW], BF16, tag="g", align_bytes=64)
             gts[m] = g_new
 
-        def sums(m, pair):
-            bank = banks[(m, pair)][:].bitcast(BF16).rearrange("p (u x e) -> p x u e", u=2, e=2)
+        def sums(m, pair, first=0):
+            bank = banks[(m, pair)][:].bitcast(BF16).rearrange("p (u x e) -> p x u e", u=2, e=2)[:, T * first :]
             for side in range(2):
-                i = 2 * side + pair % 2
-                o = GW * side + D * pair
-                nc.vector.tensor_tensor(
-                    out=gts[m][:, o : o + D].rearrange("p (x u e) -> p x u e", u=2, e=2),
-                    in0=bank,
-                    in1=bfull[:, D * i : D * i + D].rearrange("p (x u e) -> p x u e", u=2, e=2),
-                    op=ADD,
-                )
+                i = 2 * (pair % 2) + side
+                o = D * (2 * pair + side) + 512 * first
+                if m == 0:
+                    bias = bsm[:].bitcast(BF16)[:, 8 * i : 8 * i + 8].rearrange("p (g u e) -> p g u e", g=2, u=2)
+                    nc.vector.tensor_tensor(
+                        out=gts[m][:, o : o + D].rearrange("p (g r u e) -> p g r u e", g=2, u=2, e=2),
+                        in0=bank.rearrange("p (g r) u e -> p g r u e", g=2),
+                        in1=bias.unsqueeze(2).to_broadcast([P, 2, T, 2, 2]),
+                        op=ADD,
+                    )
+                else:
+                    n = D - 512 * first
+                    nc.vector.tensor_tensor(
+                        out=gts[m][:, o : o + n].rearrange("p (x u e) -> p x u e", u=2, e=2),
+                        in0=bank,
+                        in1=bfull[:, D * i + 512 * first : D * i + D].rearrange("p (x u e) -> p x u e", u=2, e=2),
+                        op=ADD,
+                    )
 
-        def sums_tail(m, side):
-            o = GW * side
+        def sums_tail(m, side, batch, heads):
+            o = GW * side + 2 * D * batch
+            w = 2 * D * batch
             nc.vector.tensor_tensor(
-                out=gts[m][:, o : o + GW].rearrange("p (b x) -> p b x", b=2),
-                in0=raws[m][:].bitcast(BF16).rearrange("p (b x) -> p b x", b=2),
-                in1=bfull[:, 2 * D * side : 2 * D * side + 2 * D].unsqueeze(1).to_broadcast([P, 2, 2 * D]),
+                out=gts[m][:, o : o + D * heads].rearrange("p (h x) -> p h x", h=heads),
+                in0=raws[m][:].bitcast(BF16)[:, w : w + D * heads].rearrange("p (h x) -> p h x", h=heads),
+                in1=bfull[:].rearrange("p (h s x) -> p s h x", h=2, s=2)[:, side, 0:heads],
                 op=ADD,
             )
 
         def sums_gpsimd(m):
-            for side in (1, 0):
-                o = GW * side + 3 * D
-                i = 2 * side + 1
+            for side in range(2):
+                o = (6 + side) * D
+                i = 2 + side
                 nc.gpsimd.tensor_tensor(
-                    out=gts[m][:, o : o + 512],
-                    in0=small[m][:].bitcast(BF16),
-                    in1=bfull[:, D * i : D * i + 512],
-                    op=ADD,
+                    out=gts[m][:, o : o + 512], in0=small[m][:].bitcast(BF16), in1=bfull[:, D * i : D * i + 512], op=ADD
                 )
+
+        def sum_part(m, dst, src, pair, side, g, u, e):
+            col = 8 * (2 * (pair % 2) + side) + 4 * g + 2 * u + e
+            nc.scalar.activation(
+                out=gts[m][:, dst : dst + 512].rearrange("p (r j) -> p r j", j=4)[:, :, 2 * u + e],
+                in_=src,
+                func=IDENTITY,
+                bias=b32[:, col : col + 1],
+                scale=1.0,
+            )
 
         def sums_scalar(m, first, last):
-            bank = shared[m][:].bitcast(BF16).rearrange("p (c r e) -> p c r e", c=4, e=2)
+            bank = shared[m][:].bitcast(BF16).rearrange("p (u g r e) -> p u g r e", u=2, g=2, e=2)
             for idx in range(first, last):
-                side = idx // 4
-                u = (idx // 2) % 2
-                e = idx % 2
-                col = 8 * (2 * side + 1) + 4 + 2 * u + e
-                o = GW * side + 3 * D + 512
-                nc.scalar.activation(
-                    out=gts[m][:, o : o + 512].rearrange("p (r j) -> p r j", j=4)[:, :, 2 * u + e],
-                    in_=bank[:, 2 * u + 1, :, e],
-                    func=IDENTITY,
-                    bias=b32[:, col : col + 1],
-                    scale=1.0,
-                )
+                side, u, e = idx // 4, (idx // 2) % 2, idx % 2
+                sum_part(m, (6 + side) * D + 512, bank[:, u, 1, :, e], 3, side, 1, u, e)
 
-        def quantise(name, m, src):
-            cq = codes.tile([P, GW // 4], U32, tag="c" + name, align_bytes=64)
-            sq = codes.tile([P, GW // 4], U8, tag="s" + name, align_bytes=64)
-            nc.vector.quantize_mx(out=cq[:].bitcast(FP8X4), scales=sq[:], in_=src)
-            cod[(name, m)] = (cq, sq)
+        def sums_scalar_tail(m, pair, first, last):
+            words = words_of(raws[m][:], pair).bitcast(BF16).rearrange("p (g r u e) -> p u g r e", g=2, u=2, e=2)
+            for idx in range(first, last):
+                g, u, e = idx // 4, (idx // 2) % 2, idx % 2
+                sum_part(m, GW + D * pair + 512 * g, words[:, u, g, :, e], pair, 1, g, u, e)
 
-        def quantise_side(m, side):
-            quantise("rw"[side], m, gts[m][:, GW * side : GW * side + GW])
+        def quantise(name, m, src, parts=1, part=0):
+            if part == 0:
+                cq = codes.tile([P, GW // 4], U32, tag="c" + name, align_bytes=64)
+                sq = codes.tile([P, GW // 4], U8, tag="s" + name, align_bytes=64)
+                cod[(name, m)] = (cq, sq)
+            cq, sq = cod[(name, m)]
+            n = GW // 4 // parts
+            nc.vector.quantize_mx(
+                out=cq[:, n * part : n * part + n].bitcast(FP8X4),
+                scales=sq[:, n * part : n * part + n],
+                in_=src[:, 4 * n * part : 4 * n * part + 4 * n],
+            )
 
-        def quantise_k(m):
-            quantise("k", m, gks[m][:])
+        def quantise_half(m, half, parts=1, part=0):
+            quantise("ab"[half], m, gts[m][:, GW * half : GW * half + GW], parts, part)
 
-        def multiply(bank, left, right, shared_right):
-            lc, ls = left
-            mc, ms = right
-            for pair in range(GROUP):
+        def quantise_k(m, parts=1, part=0):
+            quantise("k", m, gks[m][:], parts, part)
+
+        def place(m, side, pair):
+            if m < NM:
+                return cod[("ab"[pair // 2], m)] + (512 * (pair % 2) + 256 * side,)
+            return cod[("ab"[side], m)] + (256 * pair,)
+
+        def multiply(bank, m, side, right, pairs):
+            for pair in pairs:
+                lc, ls, a = place(m, side, pair)
+                mc, ms, b = right(pair)
                 for g in range(2):
-                    a = 128 * (2 * pair + g)
-                    b = 128 * (2 * (pair % 2) + g) if shared_right else a
                     nc.tensor.matmul_mx(
                         out=bank[:, 128 * pair : 128 * pair + 128],
-                        lhsT=lc[:, a : a + 128].bitcast(FP8X4),
-                        lhsT_scale=ls[:, a : a + 128],
-                        rhs=mc[:, b : b + 128].bitcast(FP8X4),
-                        rhs_scale=ms[:, b : b + 128],
+                        lhsT=lc[:, a + 128 * g : a + 128 * g + 128].bitcast(FP8X4),
+                        lhsT_scale=ls[:, a + 128 * g : a + 128 * g + 128],
+                        rhs=mc[:, b + 128 * g : b + 128 * g + 128].bitcast(FP8X4),
+                        rhs_scale=ms[:, b + 128 * g : b + 128 * g + 128],
                         start=(g == 0),
                         stop=(g == 1),
                     )
 
         def mult_rel(m):
             rel = psum.tile([P, 512], F32, tag="rel", bufs=1)
-            multiply(rel, cod[("r", m)], (rc, rs), True)
+            multiply(rel, m, 0, lambda pair: (rc, rs, 256 * (pair % 2)), range(GROUP))
             rels[m] = rel
 
-        def mult_content(m, tag="cont"):
-            cont = psum.tile([P, 512], F32, tag=tag, bufs=1)
-            multiply(cont, cod[("w", m)], cod[("k", m)], False)
-            conts[m] = cont
+        def mult_content(m, pairs=range(GROUP), tag="cont"):
+            if 0 in pairs:
+                cont = psum.tile([P, 512], F32, tag=tag, bufs=1)
+                conts[m] = cont
+            multiply(conts[m], m, 1, lambda pair: cod[("k", m)] + (256 * pair,), pairs)
 
         def area_of(m):
             base = max(B * H * T * T - GROUP * SLOT * (NG - m), 0)
@@ -311,20 +336,21 @@ def tile_relativepositionembedding_pa_t_kernel(tc, q, k, r_w_bias, r_r_bias, rel
             nc.sync.dma_start(out=rb[:], in_=area_of(m)[GROUP * T :].rearrange("(t x) -> t x", t=T))
             rbs[m] = rb
 
-        def final_add(m):
-            fin = back_pool.tile([P, GROUP * T], F32, tag="fin")
+        def final_add(m, first=0, last=GROUP):
+            if first == 0:
+                fin = back_pool.tile([P, GROUP * T], F32, tag="fin", bufs=4)
+                fins[m] = fin
             nc.vector.tensor_tensor(
-                out=fin[:].rearrange("p (i j) -> p j i", i=GROUP),
-                in0=conts[m][:].rearrange("p (i j) -> p j i", i=GROUP),
-                in1=rbs[m][:].rearrange("p (j i) -> p j i", i=GROUP),
+                out=fins[m][:].rearrange("p (i j) -> p j i", i=GROUP)[:, :, first:last],
+                in0=conts[m][:].rearrange("p (i j) -> p j i", i=GROUP)[:, :, first:last],
+                in1=rbs[m][:].rearrange("p (j i) -> p j i", i=GROUP)[:, :, first:last],
                 op=ADD,
             )
-            fins[m] = fin
 
-        def final_store(m, queue):
+        def final_store(m, queue, first=0, last=2):
             queue.dma_start(
-                out=out[2 * m : 2 * m + 2].rearrange("b h t j -> t (b h) j"),
-                in_=fins[m][:].rearrange("p (i j) -> p i j", i=GROUP),
+                out=out[2 * m + first : 2 * m + last].rearrange("b h t j -> t (b h) j"),
+                in_=fins[m][:, H * T * first : H * T * last].rearrange("p (i j) -> p i j", i=H * (last - first)),
             )
 
         for pair in range(3):
@@ -344,11 +370,11 @@ def tile_relativepositionembedding_pa_t_kernel(tc, q, k, r_w_bias, r_r_bias, rel
             if m >= 2:
                 mult_rel(m - 2)
             sums(m, 0)
-            if offloaded(m):
+            if with_gpsimd(m):
                 sums_gpsimd(m)
             turn_q(m + 1, 0)
             turn_tail(m + 1, 0)
-            if offloaded(m):
+            if with_scalar(m):
                 sums_scalar(m, 0, 8)
             if m >= 1:
                 turn_k(m, 2)
@@ -360,8 +386,8 @@ def tile_relativepositionembedding_pa_t_kernel(tc, q, k, r_w_bias, r_r_bias, rel
             sums(m, 2)
             turn_q(m + 1, 2)
             turn_tail(m + 1, 2)
-            if not offloaded(m):
-                sums(m, 3)
+            if not with_scalar(m):
+                sums(m, 3, 1 if with_gpsimd(m) else 0)
             if m >= 4:
                 final_add(m - 4)
             if m >= 3:
@@ -383,53 +409,64 @@ def tile_relativepositionembedding_pa_t_kernel(tc, q, k, r_w_bias, r_r_bias, rel
                     copy_k(0, pair)
             turn_k(m + 1, 0, 1)
             if m == 1:
-                quantise_side(0, 0)
-                quantise_side(0, 1)
+                quantise_half(0, 0)
+                quantise_half(0, 1)
                 nc.vector.quantize_mx(out=rc[:].bitcast(FP8X4), scales=rs[:], in_=gr[:])
                 quantise_k(0)
-            if m >= 2:
+            if 2 <= m < NM - 1:
                 quantise_k(m - 1)
-                quantise_side(m - 1, 0)
-                quantise_side(m - 1, 1)
+            if m >= 2:
+                quantise_half(m - 1, 0)
+                quantise_half(m - 1, 1)
 
         y, z = NM - 1, NM
         fetch(NM - 3)
-        final_store(NM - 5, nc.sync)
         new_g(z)
         copy_k(z, 0, 1)
         mult_rel(NM - 2)
         pad_rel(NM - 2)
         park(NM - 2)
-        sums_tail(z, 0)
-        turn_k(z, 2, 3)
         final_add(NM - 4)
+        sums_tail(z, 0, 0, 2)
+        sums_tail(z, 0, 1, 2)
+        turn_k(z, 2, 3)
         mult_content(NM - 3)
-        quantise_side(y, 0)
-        copy_k(z, 2, 3)
+        final_store(NM - 5, nc.scalar)
+        sums_scalar_tail(z, 3, 0, 3)
+        quantise_half(y, 0)
+        quantise_half(y, 1)
         mult_rel(y)
+        copy_k(z, 2, 3)
         pad_rel(y)
         park(y)
-        quantise_side(z, 0)
+        fetch(NM - 2)
+        quantise_half(z, 0)
         mult_rel(z)
         pad_rel(z)
-        fetch(NM - 2)
         park(z)
-        final_store(NM - 4, nc.sync)
+        fetch(y)
+        sums_scalar_tail(z, 3, 3, 8)
+        quantise_k(NM - 2)
+        final_store(NM - 4, nc.scalar)
         final_add(NM - 3)
         mult_content(NM - 2)
         quantise_k(y)
-        quantise_side(y, 1)
-        fetch(y)
-        final_store(NM - 3, nc.sync)
-        sums_tail(z, 1)
+        fetch(z)
+        sums_tail(z, 1, 0, 2)
+        sums_tail(z, 1, 1, 1)
         final_add(NM - 2)
         mult_content(y)
-        fetch(z)
-        final_store(NM - 2, nc.sync)
-        quantise_k(z)
-        quantise_side(z, 1)
-        mult_content(z, "xs")
+        final_store(NM - 3, nc.scalar)
+        final_store(NM - 2, nc.scalar)
+        quantise_k(z, 2, 0)
+        quantise_half(z, 1, 2, 0)
+        mult_content(z, (0, 1), "xs")
+        quantise_k(z, 2, 1)
+        quantise_half(z, 1, 2, 1)
+        mult_content(z, (2, 3), "xs")
         final_add(y)
-        final_store(y, nc.sync)
-        final_add(z)
-        final_store(z, nc.sync)
+        final_add(z, 0, 2)
+        final_store(y, nc.scalar)
+        final_store(z, nc.sync, 0, 1)
+        final_add(z, 2, 4)
+        final_store(z, nc.sync, 1, 2)

from contextlib import ExitStack

import concourse.mybir as mybir
from concourse.masks import make_identity

F32 = mybir.dt.float32
BF16 = mybir.dt.bfloat16
U32 = mybir.dt.uint32
U8 = mybir.dt.uint8
FP8X4 = mybir.dt.float8_e4m3fn_x4
ADD = mybir.AluOpType.add
IDENTITY = mybir.ActivationFunctionType.Identity

B, T, H, D = 32, 128, 2, 1024
P = 128
FLOPS = 2 * 2 * B * H * T * T * D

GROUP = 4
NG = B * H // GROUP
NM = NG - 1
SLOT = (T + 1) * T
NSTG = 3
PF = 3
GW = 2 * H * D


def words_of(q_words, pair):
    return q_words[:, 512 * pair : 512 * pair + 512]


def transpose_pair(nc, bank, words, ident):
    for u in range(2):
        for g in range(2):
            c = 2 * u + g
            nc.tensor.transpose(
                bank[:, 128 * c : 128 * c + 128], words[:, 256 * g + u : 256 * (g + 1) : 2], ident
            )


def leave_bank(nc, dst_words, bank):
    nc.scalar.copy(
        out=dst_words.rearrange("p (x u) -> p x u", u=2),
        in_=bank[:].rearrange("p (u x) -> p x u", u=2),
    )


def tile_relativepositionembedding_pa_t_kernel(tc, q, k, r_w_bias, r_r_bias, rel_pos_emb, out):
    nc = tc.nc
    out_flat = out.rearrange("b h t j -> (b h t j)")
    with ExitStack() as ctx:
        const = ctx.enter_context(tc.tile_pool(name="const", bufs=1))
        io = ctx.enter_context(tc.tile_pool(name="io", bufs=PF + 1))
        rawp = ctx.enter_context(tc.tile_pool(name="rawp", bufs=2))
        work = ctx.enter_context(tc.tile_pool(name="work", bufs=2))
        codes = ctx.enter_context(tc.tile_pool(name="codes", bufs=4))
        back_pool = ctx.enter_context(tc.tile_pool(name="backp", bufs=3))
        psum = ctx.enter_context(tc.psum_pool(name="psum", bufs=2))
        ctx.enter_context(tc.manual_schedule())

        brow = const.tile([P, D], BF16)
        nc.gpsimd.memset(brow[:].bitcast(F32), 0.0)
        ident = const.tile([P, P], F32)
        make_identity(nc, ident[:])

        qts = {}
        kts = {}

        def load_q(m, pieces=1):
            if m < NG:
                qt = io.tile([P, GW], BF16, tag="q")
                qts[m] = qt
                if pieces == 1:
                    nc.sync.dma_start(
                        out=qt[:].rearrange("p (b x) -> p b x", b=2),
                        in_=q[2 * m : 2 * m + 2].rearrange("b t h d -> t b (h d)"),
                    )

        def load_k(m):
            if m < NG:
                kt = io.tile([P, GW], BF16, tag="k")
                nc.sync.dma_start(
                    out=kt[:].rearrange("p (b x) -> p b x", b=2),
                    in_=k[2 * m : 2 * m + 2].rearrange("b t h d -> t b (h d)"),
                )
                kts[m] = kt

        load_q(0, pieces=2)
        nc.sync.dma_start(out=brow[0:2, :], in_=r_r_bias)
        nc.sync.dma_start(out=brow[2:4, :], in_=r_w_bias)
        nc.sync.dma_start(out=qts[0][:, 0:D], in_=q[0][:, 0, :])
        nc.sync.dma_start(out=qts[0][:, D : 2 * D], in_=q[0][:, 1, :])
        nc.sync.dma_start(out=qts[0][:, 2 * D : 4 * D], in_=q[1].rearrange("t h d -> t (h d)"))
        load_q(1)
        rsb = const.tile([P, H * D], BF16)
        nc.sync.dma_start(out=rsb[:], in_=rel_pos_emb.rearrange("j h d -> j (h d)"))
        load_k(0)
        load_k(1)
        load_q(2)
        load_k(2)

        def with_gpsimd(m):
            return 1 <= m < NM

        def with_scalar(m):
            return 3 <= m < NM - 1

        stg = []
        for s in range(NSTG):
            st = const.tile([P, GROUP * (T + 1)], F32, name="stg%d" % s)
            nc.gpsimd.memset(st[:], 0.0)
            stg.append(st)

        pb = psum.tile([P, 512], F32, tag="xk")
        brow_w = brow[:].bitcast(F32)
        for c in range(4):
            first = 256 * (c // 2) + c % 2
            nc.tensor.transpose(
                pb[:, 128 * c : 128 * c + 128], brow_w[:, first : 256 * (c // 2 + 1) : 2], ident[:]
            )
        bsm = const.tile([P, 16], F32)
        nc.vector.tensor_copy(
            out=bsm[:].rearrange("p (h s c) -> p s h c", s=2, c=4),
            in_=pb[:].rearrange("p (c i) -> p i c", c=4)[:, 0:4, :].rearrange("p (s h) c -> p s h c", s=2),
        )
        bfull = const.tile([P, 4 * D], BF16, align_bytes=64)
        bfull_w = bfull[:].bitcast(F32)

        def widen(copy, i):
            copy(
                out=bfull_w[:, 512 * i : 512 * i + 512].rearrange("p (g r u) -> p g r u", g=2, u=2),
                in_=bsm[:, 4 * i : 4 * i + 4].rearrange("p (g u) -> p g u", g=2).unsqueeze(2).to_broadcast([P, 2, T, 2]),
            )

        for i in range(4):
            widen(nc.scalar.copy, i)
        b32 = const.tile([P, 32], F32)
        nc.vector.tensor_copy(out=b32[:], in_=bsm[:].bitcast(BF16))

        gr = const.tile([P, H * D], BF16, align_bytes=64)
        rc = const.tile([P, 512], U32, align_bytes=64)
        rs = const.tile([P, 512], U8, align_bytes=64)

        def prepare_r():
            for h in range(H):
                xr = psum.tile([P, 512], F32, tag="xk")
                transpose_pair(nc, xr, words_of(rsb[:].bitcast(F32), h), ident[:])
                leave_bank(nc, words_of(gr[:].bitcast(F32), h), xr)

        banks = {}
        shared = {}
        raws = {}
        small = {}
        gts = {}
        gks = {}
        cod = {}
        rels = {}
        conts = {}
        rbs = {}
        fins = {}

        def turn_q(m, pair):
            if m < NM:
                xq = psum.tile([P, 512], F32, tag="xq", bufs=3)
                transpose_pair(nc, xq, words_of(qts[m][:].bitcast(F32), pair), ident[:])
                banks[(m, pair)] = xq

        def turn_shared(m):
            if m < NM:
                xs = psum.tile([P, 512], F32, tag="xs", bufs=1)
                transpose_pair(nc, xs, words_of(qts[m][:].bitcast(F32), 3), ident[:])
                shared[m] = xs
                banks[(m, 3)] = xs

        def copy_shared(m):
            if with_gpsimd(m):
                sm = rawp.tile([P, 256], F32, tag="small")
                nc.scalar.copy(
                    out=sm[:].rearrange("p (r u) -> p r u", u=2),
                    in_=shared[m][:].rearrange("p (u g r) -> p g r u", u=2, g=2)[:, 0],
                )
                small[m] = sm

        def turn_tail(m, pair):
            if NM <= m < NG:
                if pair == 0:
                    raw = rawp.tile([P, GW // 2], F32, tag="raw")
                    raws[m] = raw
                xq = psum.tile([P, 512], F32, tag="xq", bufs=3)
                transpose_pair(nc, xq, words_of(qts[m][:].bitcast(F32), pair), ident[:])
                leave_bank(nc, words_of(raws[m][:], pair), xq)

        def turn_k(m, *pairs):
            for pair in pairs:
                xk = psum.tile([P, 512], F32, tag="xk")
                transpose_pair(nc, xk, words_of(kts[m][:].bitcast(F32), pair), ident[:])
                banks[("k", m, pair)] = xk

        def copy_k(m, *pairs):
            if 0 in pairs:
                gk = work.tile([P, GW], BF16, tag="gk", bufs=3, align_bytes=64)
                gks[m] = gk
            for pair in pairs:
                leave_bank(nc, words_of(gks[m][:].bitcast(F32), pair), banks[("k", m, pair)])

        def new_g(m):
            g_new = work.tile([P, 2 * GW], BF16, tag="g", align_bytes=64)
            gts[m] = g_new

        def sums(m, pair, first=0):
            bank = banks[(m, pair)][:].bitcast(BF16).rearrange("p (u x e) -> p x u e", u=2, e=2)[:, T * first :]
            for side in range(2):
                i = 2 * (pair % 2) + side
                o = D * (2 * pair + side) + 512 * first
                if m == 0:
                    bias = bsm[:].bitcast(BF16)[:, 8 * i : 8 * i + 8].rearrange("p (g u e) -> p g u e", g=2, u=2)
                    nc.vector.tensor_tensor(
                        out=gts[m][:, o : o + D].rearrange("p (g r u e) -> p g r u e", g=2, u=2, e=2),
                        in0=bank.rearrange("p (g r) u e -> p g r u e", g=2),
                        in1=bias.unsqueeze(2).to_broadcast([P, 2, T, 2, 2]),
                        op=ADD,
                    )
                else:
                    n = D - 512 * first
                    nc.vector.tensor_tensor(
                        out=gts[m][:, o : o + n].rearrange("p (x u e) -> p x u e", u=2, e=2),
                        in0=bank,
                        in1=bfull[:, D * i + 512 * first : D * i + D].rearrange("p (x u e) -> p x u e", u=2, e=2),
                        op=ADD,
                    )

        def sums_tail(m, side, batch, heads):
            o = GW * side + 2 * D * batch
            w = 2 * D * batch
            nc.vector.tensor_tensor(
                out=gts[m][:, o : o + D * heads].rearrange("p (h x) -> p h x", h=heads),
                in0=raws[m][:].bitcast(BF16)[:, w : w + D * heads].rearrange("p (h x) -> p h x", h=heads),
                in1=bfull[:].rearrange("p (h s x) -> p s h x", h=2, s=2)[:, side, 0:heads],
                op=ADD,
            )

        def sums_gpsimd(m):
            for side in range(2):
                o = (6 + side) * D
                i = 2 + side
                nc.gpsimd.tensor_tensor(
                    out=gts[m][:, o : o + 512], in0=small[m][:].bitcast(BF16), in1=bfull[:, D * i : D * i + 512], op=ADD
                )

        def sum_part(m, dst, src, pair, side, g, u, e):
            col = 8 * (2 * (pair % 2) + side) + 4 * g + 2 * u + e
            nc.scalar.activation(
                out=gts[m][:, dst : dst + 512].rearrange("p (r j) -> p r j", j=4)[:, :, 2 * u + e],
                in_=src,
                func=IDENTITY,
                bias=b32[:, col : col + 1],
                scale=1.0,
            )

        def sums_scalar(m, first, last):
            bank = shared[m][:].bitcast(BF16).rearrange("p (u g r e) -> p u g r e", u=2, g=2, e=2)
            for idx in range(first, last):
                side, u, e = idx // 4, (idx // 2) % 2, idx % 2
                sum_part(m, (6 + side) * D + 512, bank[:, u, 1, :, e], 3, side, 1, u, e)

        def sums_scalar_tail(m, pair, first, last):
            words = words_of(raws[m][:], pair).bitcast(BF16).rearrange("p (g r u e) -> p u g r e", g=2, u=2, e=2)
            for idx in range(first, last):
                g, u, e = idx // 4, (idx // 2) % 2, idx % 2
                sum_part(m, GW + D * pair + 512 * g, words[:, u, g, :, e], pair, 1, g, u, e)

        def quantise(name, m, src, parts=1, part=0):
            if part == 0:
                cq = codes.tile([P, GW // 4], U32, tag="c" + name, align_bytes=64)
                sq = codes.tile([P, GW // 4], U8, tag="s" + name, align_bytes=64)
                cod[(name, m)] = (cq, sq)
            cq, sq = cod[(name, m)]
            n = GW // 4 // parts
            nc.vector.quantize_mx(
                out=cq[:, n * part : n * part + n].bitcast(FP8X4),
                scales=sq[:, n * part : n * part + n],
                in_=src[:, 4 * n * part : 4 * n * part + 4 * n],
            )

        def quantise_half(m, half, parts=1, part=0):
            quantise("ab"[half], m, gts[m][:, GW * half : GW * half + GW], parts, part)

        def quantise_k(m, parts=1, part=0):
            quantise("k", m, gks[m][:], parts, part)

        def place(m, side, pair):
            if m < NM:
                return cod[("ab"[pair // 2], m)] + (512 * (pair % 2) + 256 * side,)
            return cod[("ab"[side], m)] + (256 * pair,)

        def multiply(bank, m, side, right, pairs):
            for pair in pairs:
                lc, ls, a = place(m, side, pair)
                mc, ms, b = right(pair)
                for g in range(2):
                    nc.tensor.matmul_mx(
                        out=bank[:, 128 * pair : 128 * pair + 128],
                        lhsT=lc[:, a + 128 * g : a + 128 * g + 128].bitcast(FP8X4),
                        lhsT_scale=ls[:, a + 128 * g : a + 128 * g + 128],
                        rhs=mc[:, b + 128 * g : b + 128 * g + 128].bitcast(FP8X4),
                        rhs_scale=ms[:, b + 128 * g : b + 128 * g + 128],
                        start=(g == 0),
                        stop=(g == 1),
                    )

        def mult_rel(m):
            rel = psum.tile([P, 512], F32, tag="rel", bufs=1)
            multiply(rel, m, 0, lambda pair: (rc, rs, 256 * (pair % 2)), range(GROUP))
            rels[m] = rel

        def mult_content(m, pairs=range(GROUP), tag="cont"):
            if 0 in pairs:
                cont = psum.tile([P, 512], F32, tag=tag, bufs=1)
                conts[m] = cont
            multiply(conts[m], m, 1, lambda pair: cod[("k", m)] + (256 * pair,), pairs)

        def area_of(m):
            base = max(B * H * T * T - GROUP * SLOT * (NG - m), 0)
            return out_flat[base : base + GROUP * SLOT]

        def pad_rel(m):
            nc.scalar.copy(
                out=stg[m % NSTG][:, GROUP:].rearrange("p (j i) -> p j i", i=GROUP),
                in_=rels[m][:].rearrange("p (i j) -> p j i", i=GROUP),
            )

        def park(m):
            nc.scalar.dma_start(out=area_of(m).rearrange("(t x) -> t x", t=T), in_=stg[m % NSTG][:])

        def fetch(m):
            rb = back_pool.tile([P, GROUP * T], F32, tag="rb")
            nc.sync.dma_start(out=rb[:], in_=area_of(m)[GROUP * T :].rearrange("(t x) -> t x", t=T))
            rbs[m] = rb

        def final_add(m, first=0, last=GROUP):
            if first == 0:
                fin = back_pool.tile([P, GROUP * T], F32, tag="fin", bufs=4)
                fins[m] = fin
            nc.vector.tensor_tensor(
                out=fins[m][:].rearrange("p (i j) -> p j i", i=GROUP)[:, :, first:last],
                in0=conts[m][:].rearrange("p (i j) -> p j i", i=GROUP)[:, :, first:last],
                in1=rbs[m][:].rearrange("p (j i) -> p j i", i=GROUP)[:, :, first:last],
                op=ADD,
            )

        def final_store(m, queue, first=0, last=2):
            queue.dma_start(
                out=out[2 * m + first : 2 * m + last].rearrange("b h t j -> t (b h) j"),
                in_=fins[m][:, H * T * first : H * T * last].rearrange("p (i j) -> p i j", i=H * (last - first)),
            )

        for pair in range(3):
            turn_q(0, pair)
        turn_shared(0)
        copy_shared(0)

        for m in range(NM):
            if m > 0:
                load_q(m - 1 + PF)
                load_k(m - 1 + PF)
            if m >= 3:
                fetch(m - 3)
            new_g(m)
            if m >= 1:
                copy_k(m, 0, 1)
            if m >= 2:
                mult_rel(m - 2)
            sums(m, 0)
            if with_gpsimd(m):
                sums_gpsimd(m)
            turn_q(m + 1, 0)
            turn_tail(m + 1, 0)
            if with_scalar(m):
                sums_scalar(m, 0, 8)
            if m >= 1:
                turn_k(m, 2)
            sums(m, 1)
            turn_q(m + 1, 1)
            turn_tail(m + 1, 1)
            if m >= 1:
                turn_k(m, 3)
            sums(m, 2)
            turn_q(m + 1, 2)
            turn_tail(m + 1, 2)
            if not with_scalar(m):
                sums(m, 3, 1 if with_gpsimd(m) else 0)
            if m >= 4:
                final_add(m - 4)
            if m >= 3:
                mult_content(m - 3)
            if m >= 1:
                copy_k(m, 2, 3)
            if m >= 5:
                final_store(m - 5, nc.scalar)
            if m >= 2:
                pad_rel(m - 2)
                park(m - 2)
            turn_shared(m + 1)
            copy_shared(m + 1)
            turn_tail(m + 1, 3)
            if m == 0:
                prepare_r()
                for pair in range(GROUP):
                    turn_k(0, pair)
                    copy_k(0, pair)
            turn_k(m + 1, 0, 1)
            if m == 1:
                quantise_half(0, 0)
                quantise_half(0, 1)
                nc.vector.quantize_mx(out=rc[:].bitcast(FP8X4), scales=rs[:], in_=gr[:])
                quantise_k(0)
            if 2 <= m < NM - 1:
                quantise_k(m - 1)
            if m >= 2:
                quantise_half(m - 1, 0)
                quantise_half(m - 1, 1)

        y, z = NM - 1, NM
        fetch(NM - 3)
        new_g(z)
        copy_k(z, 0, 1)
        mult_rel(NM - 2)
        pad_rel(NM - 2)
        park(NM - 2)
        final_add(NM - 4)
        sums_tail(z, 0, 0, 2)
        sums_tail(z, 0, 1, 2)
        turn_k(z, 2, 3)
        mult_content(NM - 3)
        final_store(NM - 5, nc.scalar)
        sums_scalar_tail(z, 3, 0, 3)
        quantise_half(y, 0)
        quantise_half(y, 1)
        mult_rel(y)
        copy_k(z, 2, 3)
        pad_rel(y)
        park(y)
        fetch(NM - 2)
        quantise_half(z, 0)
        mult_rel(z)
        pad_rel(z)
        park(z)
        fetch(y)
        sums_scalar_tail(z, 3, 3, 8)
        quantise_k(NM - 2)
        final_store(NM - 4, nc.scalar)
        final_add(NM - 3)
        mult_content(NM - 2)
        quantise_k(y)
        fetch(z)
        sums_tail(z, 1, 0, 2)
        sums_tail(z, 1, 1, 1)
        final_add(NM - 2)
        mult_content(y)
        final_store(NM - 3, nc.scalar)
        final_store(NM - 2, nc.scalar)
        quantise_k(z, 2, 0)
        quantise_half(z, 1, 2, 0)
        mult_content(z, (0, 1), "xs")
        quantise_k(z, 2, 1)
        quantise_half(z, 1, 2, 1)
        mult_content(z, (2, 3), "xs")
        final_add(y)
        final_add(z, 0, 2)
        final_store(y, nc.scalar)
        final_store(z, nc.sync, 0, 1)
        final_add(z, 2, 4)
        final_store(z, nc.sync, 1, 2)
